import numpy as np
import ml_dtypes


def mxq(x, axis, fmt="e4m3"):
    dtype, down = {"e4m3": (ml_dtypes.float8_e4m3fn, 7), "e5m2": (ml_dtypes.float8_e5m2, 14)}[fmt]
    v = np.moveaxis(np.asarray(x, np.float32).astype(ml_dtypes.bfloat16).astype(np.float64), axis, -1)
    blocks = v.reshape(v.shape[:-1] + (-1, 32))
    amax = np.abs(blocks).max(-1, keepdims=True)
    byte = np.maximum(np.where(amax > 0, np.frexp(amax)[1] - 1 + 127, 0) - down, 1)
    scale = np.exp2(byte - 127.0)
    codes = (blocks / scale).astype(np.float32).astype(dtype).astype(np.float64)
    return np.moveaxis((codes * scale).reshape(v.shape), -1, axis)


WIDE = False


def mx_kscale(k):
    if not WIDE:
        return np.ones(k)
    levels = np.array([10, -10, 5, -5, 0])
    a = np.random.permutation(np.resize(levels, k // 512 * 4)).reshape(k // 512, 4)
    idx = np.arange(k)
    return np.exp2(a[idx // 512, idx % 128 // 32])


BF16 = ml_dtypes.bfloat16


def bf(x):
    return np.asarray(x, np.float32).astype(BF16)


def f64(x):
    return np.asarray(x).astype(np.float64)


E2M1 = np.array([0.0, 0.5, 1.0, 1.5, 2.0, 3.0, 4.0, 6.0, -0.0, -0.5, -1.0, -1.5, -2.0, -3.0, -4.0, -6.0])


def pack_weight(w, fmt):
    k, n = w.shape
    w = f64(bf(w)).reshape(k // 32, 32, n)
    amax = np.abs(w).max(1)
    if fmt == "e4m3":
        byte = np.frexp(amax)[1] - 1 + 127 - 7
    else:
        mant, ex = np.frexp(amax / 6.0)
        byte = np.where(mant > 0.5, ex, ex - 1) + 127
    byte = np.clip(np.where(amax > 0, byte, 1), 1, 254)
    scaled = (w * np.exp2(127.0 - byte)[:, None, :]).reshape(k, n).astype(np.float32)
    by_word = np.ascontiguousarray(scaled.reshape(k // 512, 128, 4, n).transpose(0, 1, 3, 2))
    if fmt == "e4m3":
        words = by_word.astype(ml_dtypes.float8_e4m3fn).view(np.uint8)
    else:
        c = by_word.astype(ml_dtypes.float4_e2m1fn).view(np.uint8) & 0xF
        words = c[..., 0::2] | (c[..., 1::2] << 4)
    return np.ascontiguousarray(words), np.ascontiguousarray(byte.astype(np.uint8).reshape(k // 512, 16, n))


def unpack_weight(words, scales, fmt):
    g, p, n, _ = words.shape
    if fmt == "e4m3":
        vals = np.ascontiguousarray(words).view(ml_dtypes.float8_e4m3fn).astype(np.float64)
    else:
        nib = np.empty((g, p, n, 4), np.uint8)
        nib[..., 0::2] = words & 0xF
        nib[..., 1::2] = words >> 4
        vals = E2M1[nib]
    vals = vals * np.repeat(np.exp2(scales.astype(np.float64) - 127.0), 8, axis=1)[..., None]
    return vals.transpose(0, 1, 3, 2).reshape(g * 512, n)

def pack4(w):
    words, scales = pack_weight(w, "e2m1")
    return words.reshape(words.shape[0], 128, -1), scales


def unpack4(words, scales):
    return unpack_weight(words.reshape(words.shape[0], 128, -1, 2), scales, "e2m1")


B, IN, H, OUT, DEG = 4096, 512, 512, 512, 4


def cheby(t):
    ts = [np.ones_like(t), t]
    for _ in range(DEG - 1):
        ts.append(2.0 * t * ts[-1] - ts[-2])
    return np.concatenate(ts[1:], axis=-1)


def setup_inputs():
    s = mx_kscale(IN)
    r = np.random.standard_normal
    x = bf(r((B, IN)) * s)
    w1 = r((H, IN)) / np.sqrt(IN) / s
    words, scales = pack4(np.ascontiguousarray(w1.T))
    return {"x": x,
            "w1_base_words": words,
            "w1_base_scales": scales,
            "b1_base": bf(0.2 * r(H)),
            "c1": bf(r((IN, H, DEG + 1)) * 0.5 / np.sqrt(IN)),
            "s1": bf(1.0 + 0.1 * r(H))}


def reference(x, w1_base_words, w1_base_scales, b1_base, c1, s1):
    x, c = f64(x), f64(c1)
    base = (mxq(x, 1, "e4m3") @ unpack4(w1_base_words, w1_base_scales)) + f64(b1_base)
    tcat = cheby(np.tanh(x))
    ccat = c[:, :, 1:].transpose(2, 0, 1).reshape(DEG * IN, H)
    poly = c[:, :, 0].sum(0) + (mxq(tcat, 1, "e4m3") @ mxq(ccat, 0, "e4m3"))
    return base + poly * f64(s1)

@@ -1,0 +1,317 @@
+from contextlib import ExitStack
+
+import concourse.mybir as mybir
+from concourse.masks import make_identity
+
+F32 = mybir.dt.float32
+BF16 = mybir.dt.bfloat16
+I32 = mybir.dt.int32
+U32 = mybir.dt.uint32
+U8 = mybir.dt.uint8
+FP8X4 = mybir.dt.float8_e4m3fn_x4
+FP4X4 = mybir.dt.float4_e2m1fn_x4
+ACT = mybir.ActivationFunctionType
+ALU = mybir.AluOpType
+
+P = 128
+PACK = 4
+B, IN, H, DEG = 4096, 512, 512, 4
+ROWS = 512
+SUB = ROWS // P
+N_CHUNKS = B // ROWS
+O_TILES = H // P
+GROUPED = ROWS * PACK
+N_OPERANDS = DEG + 1
+ONES_COLS = 32
+
+FLOPS = 2 * B * H * (IN + DEG * IN)
+
+
+def tile_chebykanprojector_pa_t_kernel(
+    tc, x, w1_base_words, w1_base_scales, b1_base, c1, s1, out
+):
+    nc = tc.nc
+    x_chunks = x.rearrange("(c p j) k -> c p j k", p=P, j=SUB)
+    out_chunks = out.rearrange("(c p j) o -> c p j o", p=P, j=SUB)
+    c_by_partition = c1.rearrange("(p t) o d -> p t o d", t=PACK)
+
+    with ExitStack() as ctx:
+        ctx.enter_context(tc.manual_schedule())
+        keep = ctx.enter_context(tc.tile_pool(name="keep", bufs=1))
+        work = ctx.enter_context(tc.tile_pool(name="work", bufs=2))
+        psum = ctx.enter_context(tc.psum_pool(name="psum", bufs=2))
+
+        x_sb = []
+        for c in range(N_CHUNKS):
+            x_sb.append(keep.tile([P, SUB, IN], BF16, name="x_sb%d" % c))
+        c_raw = keep.tile([P, PACK, H, DEG + 1], BF16)
+        c_codes = keep.tile([P, O_TILES, DEG, P], U32, align_bytes=64)
+        c_planes = keep.tile([P, O_TILES, DEG, P], U8, align_bytes=64)
+        w_words = keep.tile([P, 2 * H], U8, align_bytes=64)
+        w_plane = keep.tile([P, H], U8, align_bytes=64)
+        vec_rows = keep.tile([P, P], BF16)
+        vec_f32 = keep.tile([P, P], F32)
+        vec_cols = keep.tile([P, 2 * O_TILES], F32)
+        bias_cols = keep.tile([P, O_TILES], F32)
+        ident = keep.tile([P, P], F32)
+        ones = keep.tile([P, ONES_COLS], BF16)
+        warm = keep.tile([P, 1], F32)
+        b1_cols = vec_cols[:, 0:O_TILES]
+        s1_cols = vec_cols[:, O_TILES : 2 * O_TILES]
+
+        nc.vector.memset(warm[:], 0.0)
+        nc.scalar.activation(out=warm[:], in_=warm[:], func=ACT.Tanh)
+        nc.vector.memset(w_plane[:].bitcast(I32), 0)
+        nc.vector.memset(vec_rows[:], 0.0)
+        nc.vector.memset(ones[:], 1.0)
+        make_identity(nc, ident[:])
+
+        nc.sync.dma_start(out=x_sb[0][:], in_=x_chunks[0])
+        nc.sync.dma_start(out=x_sb[1][:], in_=x_chunks[1])
+        for ot in range(O_TILES):
+            o_cols = slice(ot * P, (ot + 1) * P)
+            nc.sync.dma_start(out=c_raw[:, :, o_cols, :], in_=c_by_partition[:, :, o_cols, :])
+        nc.sync.dma_start(out=w_words[:].bitcast(I32), in_=w1_base_words[0].bitcast(I32))
+        for quad in range(4):
+            nc.sync.dma_start(
+                out=w_plane[32 * quad : 32 * quad + 4, :].bitcast(I32),
+                in_=w1_base_scales[0, 4 * quad : 4 * quad + 4, :].bitcast(I32),
+            )
+        nc.sync.dma_start(out=vec_rows[0:O_TILES, :], in_=b1_base.rearrange("(r o) -> r o", o=P))
+        nc.sync.dma_start(
+            out=vec_rows[O_TILES : 2 * O_TILES, :], in_=s1.rearrange("(r o) -> r o", o=P)
+        )
+        for c in range(2, N_CHUNKS):
+            nc.sync.dma_start(out=x_sb[c][:], in_=x_chunks[c])
+
+        live = {}
+
+        def is_chunk(c):
+            return 0 <= c < N_CHUNKS
+
+        def transpose_x(c):
+            if not is_chunk(c):
+                return
+            for half in range(SUB // 2):
+                xt = psum.tile([P, 2, 2, P], F32, name="xt", tag="tp", bufs=4)
+                live[("xt%d" % half, c)] = xt
+                for jj in range(2):
+                    x_words = x_sb[c][:, 2 * half + jj, :].bitcast(F32)
+                    for u in range(2):
+                        nc.tensor.transpose(xt[:, jj, u, :], x_words[:, u : IN // 2 : 2], ident[:])
+
+        def copy_x(c, half, engine):
+            if not is_chunk(c):
+                return
+            if half == 0:
+                live[("acts0", c)] = work.tile([P, GROUPED], BF16, name="acts0", align_bytes=64)
+            words_out = live[("acts0", c)][:].bitcast(F32)[:, half * 4 * P : (half + 1) * 4 * P]
+            words_out = words_out.rearrange("p (j b u) -> p j b u", j=2, u=2)
+            words_in = live[("xt%d" % half, c)][:].rearrange("p j u b -> p j b u")
+            if engine == "vector":
+                nc.vector.tensor_copy(out=words_out, in_=words_in)
+            else:
+                nc.scalar.copy(out=words_out, in_=words_in)
+
+        def tanh(c):
+            if not is_chunk(c):
+                return
+            live[("t32", c)] = work.tile([P, GROUPED], F32, name="t32")
+            nc.scalar.activation(out=live[("t32", c)][:], in_=live[("acts0", c)][:], func=ACT.Tanh)
+
+        def square_1(c):
+            if not is_chunk(c):
+                return
+            live[("w32", c)] = work.tile([P, GROUPED], F32, name="w32")
+            nc.scalar.activation(
+                out=live[("w32", c)][:], in_=live[("t32", c)][:], func=ACT.Square, scale=2.0
+            )
+
+        def square_2(c):
+            if not is_chunk(c):
+                return
+            live[("q32", c)] = work.tile([P, GROUPED], F32, name="q32")
+            nc.scalar.activation(
+                out=live[("q32", c)][:], in_=live[("w32", c)][:], func=ACT.Square, scale=0.5, bias=-1.0
+            )
+
+        def cheby(c, d):
+            if not is_chunk(c):
+                return
+            t_d = work.tile([P, GROUPED], BF16, name="acts%d" % d, align_bytes=64)
+            live[("acts%d" % d, c)] = t_d
+            if d == 1:
+                nc.vector.tensor_copy(out=t_d[:], in_=live[("t32", c)][:])
+            elif d == 2:
+                nc.vector.tensor_scalar(
+                    out=t_d[:], in0=live[("w32", c)][:],
+                    scalar1=0.5, scalar2=-1.0, op0=ALU.mult, op1=ALU.add,
+                )
+            elif d == 3:
+                nc.vector.scalar_tensor_tensor(
+                    out=t_d[:], in0=live[("w32", c)][:], scalar=3.0, in1=live[("t32", c)][:],
+                    op0=ALU.subtract, op1=ALU.mult,
+                )
+            else:
+                nc.vector.tensor_scalar(
+                    out=t_d[:], in0=live[("q32", c)][:],
+                    scalar1=2.0, scalar2=-1.0, op0=ALU.mult, op1=ALU.add,
+                )
+
+        def quantise(c, a):
+            if not is_chunk(c):
+                return
+            if a == 0:
+                live[("codes", c)] = work.tile([P, N_OPERANDS, ROWS], U32, name="codes", align_bytes=64)
+                live[("planes", c)] = work.tile([P, N_OPERANDS, ROWS], U8, name="planes", align_bytes=64)
+            nc.vector.quantize_mx(
+                out=live[("codes", c)][:, a, :].bitcast(FP8X4),
+                scales=live[("planes", c)][:, a, :],
+                in_=live[("acts%d" % a, c)][:],
+            )
+
+        def multiply(c, ot):
+            if not is_chunk(c):
+                return
+            codes = live[("codes", c)]
+            planes = live[("planes", c)]
+            base_ps = psum.tile([P, ROWS], F32, name="base_ps")
+            poly_ps = psum.tile([P, ROWS], F32, name="poly_ps")
+            live[("base_ps", c)] = base_ps
+            live[("poly_ps", c)] = poly_ps
+            nc.tensor.matmul_mx(
+                out=base_ps[:],
+                lhsT=w_words[:, 2 * P * ot : 2 * P * (ot + 1)].bitcast(FP4X4),
+                lhsT_scale=w_plane[:, ot * P : (ot + 1) * P],
+                rhs=codes[:, 0, :].bitcast(FP8X4),
+                rhs_scale=planes[:, 0, :],
+                start=True,
+                stop=True,
+            )
+            for d in range(DEG):
+                nc.tensor.matmul_mx(
+                    out=poly_ps[:],
+                    lhsT=c_codes[:, ot, d, :].bitcast(FP8X4),
+                    lhsT_scale=c_planes[:, ot, d, :],
+                    rhs=codes[:, d + 1, :].bitcast(FP8X4),
+                    rhs_scale=planes[:, d + 1, :],
+                    start=(d == 0),
+                    stop=(d == DEG - 1),
+                )
+
+        def add_bias(c, ot):
+            if not is_chunk(c):
+                return
+            base_sb = work.tile([P, ROWS], F32, name="base_sb")
+            live[("base_sb", c)] = base_sb
+            nc.scalar.activation(
+                out=base_sb[:], in_=live[("base_ps", c)][:], func=ACT.Identity,
+                bias=bias_cols[:, ot : ot + 1], scale=1.0,
+            )
+
+        def combine(c, ot):
+            if not is_chunk(c):
+                return
+            if ot == 0:
+                live[("sum_t", c)] = work.tile([P, O_TILES, ROWS], F32, name="sum_t")
+            nc.vector.scalar_tensor_tensor(
+                out=live[("sum_t", c)][:, ot, :],
+                in0=live[("poly_ps", c)][:],
+                scalar=s1_cols[:, ot : ot + 1],
+                in1=live[("base_sb", c)][:],
+                op0=ALU.mult,
+                op1=ALU.add,
+            )
+
+        def finish(c, j):
+            if not is_chunk(c):
+                return
+            if j == 0:
+                live[("out_sb", c)] = work.tile([P, SUB, H], F32, name="out_sb")
+            out_ps = psum.tile([P, H], F32, name="out_ps", tag="tp", bufs=4)
+            for ot in range(O_TILES):
+                nc.tensor.transpose(
+                    out_ps[:, ot * P : (ot + 1) * P],
+                    live[("sum_t", c)][:, ot, j * P : (j + 1) * P],
+                    ident[:],
+                )
+            nc.scalar.copy(out=live[("out_sb", c)][:, j, :], in_=out_ps[:])
+            if j == SUB - 1:
+                nc.sync.dma_start(out=out_chunks[c], in_=live[("out_sb", c)][:])
+
+        def prepare_c(ot):
+            c_grouped = work.tile([P, DEG, P, PACK], BF16, name="c_grouped", align_bytes=64)
+            c_view = c_raw[:, :, ot * P : (ot + 1) * P, 1 : DEG + 1].rearrange("p t o d -> p d o t")
+            for d in range(DEG):
+                if ot % 2 == 0:
+                    nc.scalar.copy(out=c_grouped[:, d], in_=c_view[:, d])
+                else:
+                    nc.vector.tensor_copy(out=c_grouped[:, d], in_=c_view[:, d])
+            nc.vector.quantize_mx(
+                out=c_codes[:, ot].rearrange("p d o -> p (d o)").bitcast(FP8X4),
+                scales=c_planes[:, ot].rearrange("p d o -> p (d o)"),
+                in_=c_grouped[:].rearrange("p d o t -> p (d o t)"),
+            )
+
+        def prepare_vectors():
+            nc.vector.tensor_copy(out=vec_f32[:], in_=vec_rows[:])
+            vec_ps = psum.tile([P, P], F32, name="vec_ps", tag="tp", bufs=4)
+            nc.tensor.transpose(vec_ps[:], vec_f32[:], ident[:])
+            nc.vector.tensor_copy(out=vec_cols[:], in_=vec_ps[:, 0 : 2 * O_TILES])
+            c0_ps = psum.tile([P, O_TILES, ONES_COLS], F32, name="c0_ps", tag="tp", bufs=4)
+            for ot in range(O_TILES):
+                for t in range(PACK):
+                    nc.tensor.matmul(
+                        out=c0_ps[:, ot, :],
+                        lhsT=c_raw[:, t, ot * P : (ot + 1) * P, 0],
+                        rhs=ones[:],
+                        start=(t == 0),
+                        stop=(t == PACK - 1),
+                    )
+            nc.vector.tensor_tensor(out=bias_cols[:], in0=c0_ps[:, :, 0], in1=s1_cols, op=ALU.mult)
+            nc.vector.tensor_tensor(out=bias_cols[:], in0=bias_cols[:], in1=b1_cols, op=ALU.add)
+
+        for s in range(-3, N_CHUNKS + 1):
+            quantise(s, 3)
+            quantise(s, 4)
+            multiply(s, 0)
+            copy_x(s + 2, 0, "vector")
+            tanh(s + 1)
+            add_bias(s, 0)
+            finish(s - 1, 0)
+            copy_x(s + 2, 1, "scalar")
+            cheby(s + 1, 1)
+            combine(s, 0)
+            if s == -1:
+                prepare_c(0)
+            quantise(s + 1, 0)
+            quantise(s + 1, 1)
+
+            multiply(s, 1)
+            square_1(s + 1)
+            add_bias(s, 1)
+            finish(s - 1, 1)
+            cheby(s + 1, 2)
+            combine(s, 1)
+            if s == -1:
+                prepare_c(1)
+            cheby(s + 1, 3)
+            quantise(s + 1, 2)
+
+            multiply(s, 2)
+            transpose_x(s + 3)
+            square_2(s + 1)
+            add_bias(s, 2)
+            finish(s - 1, 2)
+            combine(s, 2)
+            if s == -1:
+                prepare_c(2)
+            cheby(s + 1, 4)
+
+            multiply(s, 3)
+            add_bias(s, 3)
+            finish(s - 1, 3)
+            combine(s, 3)
+            if s == -1:
+                prepare_c(3)
+                prepare_vectors()

@@ -38,6 +38,7 @@ def tile_chebykanprojector_pa_t_kernel(
     with ExitStack() as ctx:
         ctx.enter_context(tc.manual_schedule())
         keep = ctx.enter_context(tc.tile_pool(name="keep", bufs=1))
+        once = ctx.enter_context(tc.tile_pool(name="once", bufs=1))
         work = ctx.enter_context(tc.tile_pool(name="work", bufs=2))
         psum = ctx.enter_context(tc.psum_pool(name="psum", bufs=2))
 
@@ -45,6 +46,11 @@ def tile_chebykanprojector_pa_t_kernel(
         for c in range(N_CHUNKS):
             x_sb.append(keep.tile([P, SUB, IN], BF16, name="x_sb%d" % c))
         c_raw = keep.tile([P, PACK, H, DEG + 1], BF16)
+        c_grouped = []
+        for ot in range(O_TILES):
+            c_grouped.append(
+                keep.tile([P, DEG, P, PACK], BF16, name="c_grouped%d" % ot, align_bytes=64)
+            )
         c_codes = keep.tile([P, O_TILES, DEG, P], U32, align_bytes=64)
         c_planes = keep.tile([P, O_TILES, DEG, P], U8, align_bytes=64)
         w_words = keep.tile([P, 2 * H], U8, align_bytes=64)
@@ -68,6 +74,10 @@ def tile_chebykanprojector_pa_t_kernel(
 
         nc.sync.dma_start(out=x_sb[0][:], in_=x_chunks[0])
         nc.sync.dma_start(out=x_sb[1][:], in_=x_chunks[1])
+        nc.sync.dma_start(out=vec_rows[0:O_TILES, :], in_=b1_base.rearrange("(r o) -> r o", o=P))
+        nc.sync.dma_start(
+            out=vec_rows[O_TILES : 2 * O_TILES, :], in_=s1.rearrange("(r o) -> r o", o=P)
+        )
         for ot in range(O_TILES):
             o_cols = slice(ot * P, (ot + 1) * P)
             nc.sync.dma_start(out=c_raw[:, :, o_cols, :], in_=c_by_partition[:, :, o_cols, :])
@@ -77,10 +87,6 @@ def tile_chebykanprojector_pa_t_kernel(
                 out=w_plane[32 * quad : 32 * quad + 4, :].bitcast(I32),
                 in_=w1_base_scales[0, 4 * quad : 4 * quad + 4, :].bitcast(I32),
             )
-        nc.sync.dma_start(out=vec_rows[0:O_TILES, :], in_=b1_base.rearrange("(r o) -> r o", o=P))
-        nc.sync.dma_start(
-            out=vec_rows[O_TILES : 2 * O_TILES, :], in_=s1.rearrange("(r o) -> r o", o=P)
-        )
         for c in range(2, N_CHUNKS):
             nc.sync.dma_start(out=x_sb[c][:], in_=x_chunks[c])
 
@@ -94,7 +100,7 @@ def tile_chebykanprojector_pa_t_kernel(
                 return
             for half in range(SUB // 2):
                 xt = psum.tile([P, 2, 2, P], F32, name="xt", tag="tp", bufs=4)
-                live[("xt%d" % half, c)] = xt
+                live[("xt", c, half)] = xt
                 for jj in range(2):
                     x_words = x_sb[c][:, 2 * half + jj, :].bitcast(F32)
                     for u in range(2):
@@ -104,10 +110,10 @@ def tile_chebykanprojector_pa_t_kernel(
             if not is_chunk(c):
                 return
             if half == 0:
-                live[("acts0", c)] = work.tile([P, GROUPED], BF16, name="acts0", align_bytes=64)
+                live[("acts0", c)] = once.tile([P, GROUPED], BF16, name="acts0", align_bytes=64)
             words_out = live[("acts0", c)][:].bitcast(F32)[:, half * 4 * P : (half + 1) * 4 * P]
             words_out = words_out.rearrange("p (j b u) -> p j b u", j=2, u=2)
-            words_in = live[("xt%d" % half, c)][:].rearrange("p j u b -> p j b u")
+            words_in = live[("xt", c, half)][:].rearrange("p j u b -> p j b u")
             if engine == "vector":
                 nc.vector.tensor_copy(out=words_out, in_=words_in)
             else:
@@ -138,7 +144,7 @@ def tile_chebykanprojector_pa_t_kernel(
         def cheby(c, d):
             if not is_chunk(c):
                 return
-            t_d = work.tile([P, GROUPED], BF16, name="acts%d" % d, align_bytes=64)
+            t_d = once.tile([P, GROUPED], BF16, name="acts%d" % d, align_bytes=64)
             live[("acts%d" % d, c)] = t_d
             if d == 1:
                 nc.vector.tensor_copy(out=t_d[:], in_=live[("t32", c)][:])
@@ -177,8 +183,8 @@ def tile_chebykanprojector_pa_t_kernel(
             planes = live[("planes", c)]
             base_ps = psum.tile([P, ROWS], F32, name="base_ps")
             poly_ps = psum.tile([P, ROWS], F32, name="poly_ps")
-            live[("base_ps", c)] = base_ps
-            live[("poly_ps", c)] = poly_ps
+            live[("base_ps", c, ot)] = base_ps
+            live[("poly_ps", c, ot)] = poly_ps
             nc.tensor.matmul_mx(
                 out=base_ps[:],
                 lhsT=w_words[:, 2 * P * ot : 2 * P * (ot + 1)].bitcast(FP4X4),
@@ -203,9 +209,9 @@ def tile_chebykanprojector_pa_t_kernel(
             if not is_chunk(c):
                 return
             base_sb = work.tile([P, ROWS], F32, name="base_sb")
-            live[("base_sb", c)] = base_sb
+            live[("base_sb", c, ot)] = base_sb
             nc.scalar.activation(
-                out=base_sb[:], in_=live[("base_ps", c)][:], func=ACT.Identity,
+                out=base_sb[:], in_=live[("base_ps", c, ot)][:], func=ACT.Identity,
                 bias=bias_cols[:, ot : ot + 1], scale=1.0,
             )
 
@@ -216,9 +222,9 @@ def tile_chebykanprojector_pa_t_kernel(
                 live[("sum_t", c)] = work.tile([P, O_TILES, ROWS], F32, name="sum_t")
             nc.vector.scalar_tensor_tensor(
                 out=live[("sum_t", c)][:, ot, :],
-                in0=live[("poly_ps", c)][:],
+                in0=live[("poly_ps", c, ot)][:],
                 scalar=s1_cols[:, ot : ot + 1],
-                in1=live[("base_sb", c)][:],
+                in1=live[("base_sb", c, ot)][:],
                 op0=ALU.mult,
                 op1=ALU.add,
             )
@@ -236,29 +242,29 @@ def tile_chebykanprojector_pa_t_kernel(
                     ident[:],
                 )
             nc.scalar.copy(out=live[("out_sb", c)][:, j, :], in_=out_ps[:])
-            if j == SUB - 1:
-                nc.sync.dma_start(out=out_chunks[c], in_=live[("out_sb", c)][:])
+            nc.sync.dma_start(out=out_chunks[c][:, j, :], in_=live[("out_sb", c)][:, j, :])
 
-        def prepare_c(ot):
-            c_grouped = work.tile([P, DEG, P, PACK], BF16, name="c_grouped", align_bytes=64)
-            c_view = c_raw[:, :, ot * P : (ot + 1) * P, 1 : DEG + 1].rearrange("p t o d -> p d o t")
-            for d in range(DEG):
-                if ot % 2 == 0:
-                    nc.scalar.copy(out=c_grouped[:, d], in_=c_view[:, d])
-                else:
-                    nc.vector.tensor_copy(out=c_grouped[:, d], in_=c_view[:, d])
+        def regroup_c(ot):
+            nc.gpsimd.tensor_scalar(
+                out=c_grouped[ot][:],
+                in0=c_raw[:, :, ot * P : (ot + 1) * P, 1 : DEG + 1].rearrange("p t o d -> p d o t"),
+                scalar1=1.0, scalar2=0.0, op0=ALU.mult, op1=ALU.add,
+            )
+
+        def quantise_c(ot):
             nc.vector.quantize_mx(
                 out=c_codes[:, ot].rearrange("p d o -> p (d o)").bitcast(FP8X4),
                 scales=c_planes[:, ot].rearrange("p d o -> p (d o)"),
-                in_=c_grouped[:].rearrange("p d o t -> p (d o t)"),
+                in_=c_grouped[ot][:].rearrange("p d o t -> p (d o t)"),
             )
 
-        def prepare_vectors():
+        def sum_vectors():
             nc.vector.tensor_copy(out=vec_f32[:], in_=vec_rows[:])
             vec_ps = psum.tile([P, P], F32, name="vec_ps", tag="tp", bufs=4)
+            live[("vec_ps", 0)] = vec_ps
             nc.tensor.transpose(vec_ps[:], vec_f32[:], ident[:])
-            nc.vector.tensor_copy(out=vec_cols[:], in_=vec_ps[:, 0 : 2 * O_TILES])
             c0_ps = psum.tile([P, O_TILES, ONES_COLS], F32, name="c0_ps", tag="tp", bufs=4)
+            live[("c0_ps", 0)] = c0_ps
             for ot in range(O_TILES):
                 for t in range(PACK):
                     nc.tensor.matmul(
@@ -268,50 +274,58 @@ def tile_chebykanprojector_pa_t_kernel(
                         start=(t == 0),
                         stop=(t == PACK - 1),
                     )
-            nc.vector.tensor_tensor(out=bias_cols[:], in0=c0_ps[:, :, 0], in1=s1_cols, op=ALU.mult)
+
+        def make_bias():
+            nc.vector.tensor_copy(out=vec_cols[:], in_=live[("vec_ps", 0)][:, 0 : 2 * O_TILES])
+            nc.vector.tensor_tensor(
+                out=bias_cols[:], in0=live[("c0_ps", 0)][:, :, 0], in1=s1_cols, op=ALU.mult
+            )
             nc.vector.tensor_tensor(out=bias_cols[:], in0=bias_cols[:], in1=b1_cols, op=ALU.add)
 
-        for s in range(-3, N_CHUNKS + 1):
-            quantise(s, 3)
-            quantise(s, 4)
-            multiply(s, 0)
-            copy_x(s + 2, 0, "vector")
-            tanh(s + 1)
-            add_bias(s, 0)
-            finish(s - 1, 0)
-            copy_x(s + 2, 1, "scalar")
-            cheby(s + 1, 1)
-            combine(s, 0)
-            if s == -1:
-                prepare_c(0)
-            quantise(s + 1, 0)
-            quantise(s + 1, 1)
+        for ot in range(O_TILES):
+            regroup_c(ot)
 
-            multiply(s, 1)
-            square_1(s + 1)
-            add_bias(s, 1)
-            finish(s - 1, 1)
-            cheby(s + 1, 2)
-            combine(s, 1)
-            if s == -1:
-                prepare_c(1)
-            cheby(s + 1, 3)
-            quantise(s + 1, 2)
+        for p in range(-1, N_CHUNKS + 3):
+            tanh(p)
+            cheby(p - 1, 3)
+            multiply(p - 2, 2)
+            add_bias(p - 2, 2)
+            finish(p - 3, 2)
+            combine(p - 2, 1)
+            cheby(p, 1)
+            quantise(p - 1, 2)
+            cheby(p - 1, 4)
 
-            multiply(s, 2)
-            transpose_x(s + 3)
-            square_2(s + 1)
-            add_bias(s, 2)
-            finish(s - 1, 2)
-            combine(s, 2)
-            if s == -1:
-                prepare_c(2)
-            cheby(s + 1, 4)
+            multiply(p - 2, 3)
+            square_1(p)
+            add_bias(p - 2, 3)
+            finish(p - 3, 3)
+            combine(p - 2, 2)
+            quantise(p - 1, 3)
+            quantise(p, 0)
+            quantise(p - 1, 4)
+            if p == 1:
+                quantise_c(0)
+                quantise_c(1)
+                make_bias()
 
-            multiply(s, 3)
-            add_bias(s, 3)
-            finish(s - 1, 3)
-            combine(s, 3)
-            if s == -1:
-                prepare_c(3)
-                prepare_vectors()
+            transpose_x(p + 1)
+            if p == 0:
+                sum_vectors()
+            multiply(p - 1, 0)
+            square_2(p)
+            add_bias(p - 1, 0)
+            combine(p - 2, 3)
+            finish(p - 2, 0)
+            cheby(p, 2)
+            quantise(p, 1)
+
+            multiply(p - 1, 1)
+            add_bias(p - 1, 1)
+            finish(p - 2, 1)
+            if p == 1:
+                quantise_c(2)
+                quantise_c(3)
+            copy_x(p + 1, 0, "vector")
+            copy_x(p + 1, 1, "scalar")
+            combine(p - 1, 0)

@@ -38,8 +38,8 @@ def tile_chebykanprojector_pa_t_kernel(
     with ExitStack() as ctx:
         ctx.enter_context(tc.manual_schedule())
         keep = ctx.enter_context(tc.tile_pool(name="keep", bufs=1))
-        once = ctx.enter_context(tc.tile_pool(name="once", bufs=1))
-        work = ctx.enter_context(tc.tile_pool(name="work", bufs=2))
+        single = ctx.enter_context(tc.tile_pool(name="single", bufs=1))
+        double = ctx.enter_context(tc.tile_pool(name="double", bufs=2))
         psum = ctx.enter_context(tc.psum_pool(name="psum", bufs=2))
 
         x_sb = []
@@ -72,15 +72,20 @@ def tile_chebykanprojector_pa_t_kernel(
         nc.vector.memset(ones[:], 1.0)
         make_identity(nc, ident[:])
 
+        def load_c(ot):
+            o_cols = slice(ot * P, (ot + 1) * P)
+            nc.sync.dma_start(out=c_raw[:, :, o_cols, :], in_=c_by_partition[:, :, o_cols, :])
+
         nc.sync.dma_start(out=x_sb[0][:], in_=x_chunks[0])
+        load_c(0)
+        load_c(1)
         nc.sync.dma_start(out=x_sb[1][:], in_=x_chunks[1])
         nc.sync.dma_start(out=vec_rows[0:O_TILES, :], in_=b1_base.rearrange("(r o) -> r o", o=P))
         nc.sync.dma_start(
             out=vec_rows[O_TILES : 2 * O_TILES, :], in_=s1.rearrange("(r o) -> r o", o=P)
         )
-        for ot in range(O_TILES):
-            o_cols = slice(ot * P, (ot + 1) * P)
-            nc.sync.dma_start(out=c_raw[:, :, o_cols, :], in_=c_by_partition[:, :, o_cols, :])
+        load_c(2)
+        load_c(3)
         nc.sync.dma_start(out=w_words[:].bitcast(I32), in_=w1_base_words[0].bitcast(I32))
         for quad in range(4):
             nc.sync.dma_start(
@@ -110,8 +115,8 @@ def tile_chebykanprojector_pa_t_kernel(
             if not is_chunk(c):
                 return
             if half == 0:
-                live[("acts0", c)] = once.tile([P, GROUPED], BF16, name="acts0", align_bytes=64)
-            words_out = live[("acts0", c)][:].bitcast(F32)[:, half * 4 * P : (half + 1) * 4 * P]
+                live[("x_t1", c)] = double.tile([P, 2, GROUPED], BF16, name="x_t1", align_bytes=64)
+            words_out = live[("x_t1", c)][:, 0, :].bitcast(F32)[:, half * 4 * P : (half + 1) * 4 * P]
             words_out = words_out.rearrange("p (j b u) -> p j b u", j=2, u=2)
             words_in = live[("xt", c, half)][:].rearrange("p j u b -> p j b u")
             if engine == "vector":
@@ -122,13 +127,13 @@ def tile_chebykanprojector_pa_t_kernel(
         def tanh(c):
             if not is_chunk(c):
                 return
-            live[("t32", c)] = work.tile([P, GROUPED], F32, name="t32")
-            nc.scalar.activation(out=live[("t32", c)][:], in_=live[("acts0", c)][:], func=ACT.Tanh)
+            live[("t32", c)] = double.tile([P, GROUPED], F32, name="t32")
+            nc.scalar.activation(out=live[("t32", c)][:], in_=live[("x_t1", c)][:, 0, :], func=ACT.Tanh)
 
         def square_1(c):
             if not is_chunk(c):
                 return
-            live[("w32", c)] = work.tile([P, GROUPED], F32, name="w32")
+            live[("w32", c)] = double.tile([P, GROUPED], F32, name="w32")
             nc.scalar.activation(
                 out=live[("w32", c)][:], in_=live[("t32", c)][:], func=ACT.Square, scale=2.0
             )
@@ -136,44 +141,53 @@ def tile_chebykanprojector_pa_t_kernel(
         def square_2(c):
             if not is_chunk(c):
                 return
-            live[("q32", c)] = work.tile([P, GROUPED], F32, name="q32")
+            live[("q32", c)] = double.tile([P, GROUPED], F32, name="q32")
             nc.scalar.activation(
                 out=live[("q32", c)][:], in_=live[("w32", c)][:], func=ACT.Square, scale=0.5, bias=-1.0
             )
 
-        def cheby(c, d):
+        def cheby_1(c):
             if not is_chunk(c):
                 return
-            t_d = once.tile([P, GROUPED], BF16, name="acts%d" % d, align_bytes=64)
-            live[("acts%d" % d, c)] = t_d
-            if d == 1:
-                nc.vector.tensor_copy(out=t_d[:], in_=live[("t32", c)][:])
-            elif d == 2:
-                nc.vector.tensor_scalar(
-                    out=t_d[:], in0=live[("w32", c)][:],
-                    scalar1=0.5, scalar2=-1.0, op0=ALU.mult, op1=ALU.add,
-                )
-            elif d == 3:
-                nc.vector.scalar_tensor_tensor(
-                    out=t_d[:], in0=live[("w32", c)][:], scalar=3.0, in1=live[("t32", c)][:],
-                    op0=ALU.subtract, op1=ALU.mult,
-                )
-            else:
-                nc.vector.tensor_scalar(
-                    out=t_d[:], in0=live[("q32", c)][:],
-                    scalar1=2.0, scalar2=-1.0, op0=ALU.mult, op1=ALU.add,
-                )
+            nc.vector.tensor_copy(out=live[("x_t1", c)][:, 1, :], in_=live[("t32", c)][:])
 
-        def quantise(c, a):
+        def cheby_2(c):
             if not is_chunk(c):
                 return
-            if a == 0:
-                live[("codes", c)] = work.tile([P, N_OPERANDS, ROWS], U32, name="codes", align_bytes=64)
-                live[("planes", c)] = work.tile([P, N_OPERANDS, ROWS], U8, name="planes", align_bytes=64)
+            live[("t2", c)] = single.tile([P, GROUPED], BF16, name="t2", align_bytes=64)
+            nc.vector.tensor_scalar(
+                out=live[("t2", c)][:], in0=live[("w32", c)][:],
+                scalar1=0.5, scalar2=-1.0, op0=ALU.mult, op1=ALU.add,
+            )
+
+        def cheby_3(c):
+            if not is_chunk(c):
+                return
+            live[("t3_t4", c)] = single.tile([P, 2, GROUPED], BF16, name="t3_t4", align_bytes=64)
+            nc.vector.scalar_tensor_tensor(
+                out=live[("t3_t4", c)][:, 0, :], in0=live[("w32", c)][:], scalar=3.0,
+                in1=live[("t32", c)][:], op0=ALU.subtract, op1=ALU.mult,
+            )
+
+        def cheby_4(c):
+            if not is_chunk(c):
+                return
+            nc.vector.tensor_scalar(
+                out=live[("t3_t4", c)][:, 1, :], in0=live[("q32", c)][:],
+                scalar1=2.0, scalar2=-1.0, op0=ALU.mult, op1=ALU.add,
+            )
+
+        def quantise(c, name, first, count):
+            if not is_chunk(c):
+                return
+            if first == 0:
+                live[("codes", c)] = double.tile([P, N_OPERANDS, ROWS], U32, name="codes", align_bytes=64)
+                live[("planes", c)] = double.tile([P, N_OPERANDS, ROWS], U8, name="planes", align_bytes=64)
+            which = slice(first, first + count)
             nc.vector.quantize_mx(
-                out=live[("codes", c)][:, a, :].bitcast(FP8X4),
-                scales=live[("planes", c)][:, a, :],
-                in_=live[("acts%d" % a, c)][:],
+                out=live[("codes", c)][:, which, :].rearrange("p a r -> p (a r)").bitcast(FP8X4),
+                scales=live[("planes", c)][:, which, :].rearrange("p a r -> p (a r)"),
+                in_=live[(name, c)][:].rearrange("p a g -> p (a g)") if count > 1 else live[(name, c)][:],
             )
 
         def multiply(c, ot):
@@ -208,7 +222,7 @@ def tile_chebykanprojector_pa_t_kernel(
         def add_bias(c, ot):
             if not is_chunk(c):
                 return
-            base_sb = work.tile([P, ROWS], F32, name="base_sb")
+            base_sb = double.tile([P, ROWS], F32, name="base_sb")
             live[("base_sb", c, ot)] = base_sb
             nc.scalar.activation(
                 out=base_sb[:], in_=live[("base_ps", c, ot)][:], func=ACT.Identity,
@@ -219,7 +233,7 @@ def tile_chebykanprojector_pa_t_kernel(
             if not is_chunk(c):
                 return
             if ot == 0:
-                live[("sum_t", c)] = work.tile([P, O_TILES, ROWS], F32, name="sum_t")
+                live[("sum_t", c)] = double.tile([P, O_TILES, ROWS], F32, name="sum_t")
             nc.vector.scalar_tensor_tensor(
                 out=live[("sum_t", c)][:, ot, :],
                 in0=live[("poly_ps", c, ot)][:],
@@ -229,27 +243,32 @@ def tile_chebykanprojector_pa_t_kernel(
                 op1=ALU.add,
             )
 
-        def finish(c, j):
+        def transpose_out(c, j):
             if not is_chunk(c):
                 return
-            if j == 0:
-                live[("out_sb", c)] = work.tile([P, SUB, H], F32, name="out_sb")
             out_ps = psum.tile([P, H], F32, name="out_ps", tag="tp", bufs=4)
+            live[("out_ps", c, j)] = out_ps
             for ot in range(O_TILES):
                 nc.tensor.transpose(
                     out_ps[:, ot * P : (ot + 1) * P],
                     live[("sum_t", c)][:, ot, j * P : (j + 1) * P],
                     ident[:],
                 )
-            nc.scalar.copy(out=live[("out_sb", c)][:, j, :], in_=out_ps[:])
+
+        def copy_out(c, j):
+            if not is_chunk(c):
+                return
+            if j == 0:
+                live[("out_sb", c)] = double.tile([P, SUB, H], F32, name="out_sb")
+            nc.scalar.copy(out=live[("out_sb", c)][:, j, :], in_=live[("out_ps", c, j)][:])
             nc.sync.dma_start(out=out_chunks[c][:, j, :], in_=live[("out_sb", c)][:, j, :])
 
-        def regroup_c(ot):
-            nc.gpsimd.tensor_scalar(
-                out=c_grouped[ot][:],
-                in0=c_raw[:, :, ot * P : (ot + 1) * P, 1 : DEG + 1].rearrange("p t o d -> p d o t"),
-                scalar1=1.0, scalar2=0.0, op0=ALU.mult, op1=ALU.add,
-            )
+        def regroup_c(ot, engine):
+            c_view = c_raw[:, :, ot * P : (ot + 1) * P, 1 : DEG + 1].rearrange("p t o d -> p d o t")
+            if engine == "vector":
+                nc.vector.tensor_copy(out=c_grouped[ot][:], in_=c_view)
+            else:
+                nc.scalar.copy(out=c_grouped[ot][:], in_=c_view)
 
         def quantise_c(ot):
             nc.vector.quantize_mx(
@@ -282,50 +301,57 @@ def tile_chebykanprojector_pa_t_kernel(
             )
             nc.vector.tensor_tensor(out=bias_cols[:], in0=bias_cols[:], in1=b1_cols, op=ALU.add)
 
-        for ot in range(O_TILES):
-            regroup_c(ot)
-
-        for p in range(-1, N_CHUNKS + 3):
+        for p in range(-2, N_CHUNKS + 3):
+            transpose_out(p - 3, 2)
+            transpose_out(p - 3, 3)
+            transpose_x(p + 1)
+            if p == 1:
+                regroup_c(2, "scalar")
             tanh(p)
-            cheby(p - 1, 3)
+            cheby_3(p - 1)
             multiply(p - 2, 2)
+            copy_out(p - 3, 2)
             add_bias(p - 2, 2)
-            finish(p - 3, 2)
             combine(p - 2, 1)
-            cheby(p, 1)
-            quantise(p - 1, 2)
-            cheby(p - 1, 4)
+            cheby_1(p)
+            if p == 0:
+                regroup_c(1, "vector")
+                quantise_c(1)
+            if p == 1:
+                make_bias()
+            quantise(p - 1, "t2", 2, 1)
+            cheby_4(p - 1)
 
             multiply(p - 2, 3)
             square_1(p)
             add_bias(p - 2, 3)
-            finish(p - 3, 3)
+            copy_out(p - 3, 3)
             combine(p - 2, 2)
-            quantise(p - 1, 3)
-            quantise(p, 0)
-            quantise(p - 1, 4)
-            if p == 1:
+            quantise(p, "x_t1", 0, 2)
+            copy_x(p + 1, 0, "vector")
+            copy_x(p + 1, 1, "scalar")
+            quantise(p - 1, "t3_t4", 3, 2)
+            if p == -1:
+                regroup_c(0, "vector")
                 quantise_c(0)
-                quantise_c(1)
-                make_bias()
-
-            transpose_x(p + 1)
             if p == 0:
                 sum_vectors()
+            if p == 1:
+                quantise_c(2)
+                regroup_c(3, "scalar")
+
             multiply(p - 1, 0)
             square_2(p)
             add_bias(p - 1, 0)
             combine(p - 2, 3)
-            finish(p - 2, 0)
-            cheby(p, 2)
-            quantise(p, 1)
+            transpose_out(p - 2, 0)
+            copy_out(p - 2, 0)
+            transpose_out(p - 2, 1)
+            copy_out(p - 2, 1)
+            cheby_2(p)
 
             multiply(p - 1, 1)
             add_bias(p - 1, 1)
-            finish(p - 2, 1)
             if p == 1:
-                quantise_c(2)
                 quantise_c(3)
-            copy_x(p + 1, 0, "vector")
-            copy_x(p + 1, 1, "scalar")
             combine(p - 1, 0)

@@ -76,7 +76,9 @@ def tile_chebykanprojector_pa_t_kernel(
             o_cols = slice(ot * P, (ot + 1) * P)
             nc.sync.dma_start(out=c_raw[:, :, o_cols, :], in_=c_by_partition[:, :, o_cols, :])
 
-        nc.sync.dma_start(out=x_sb[0][:], in_=x_chunks[0])
+        for half in range(2):
+            rows = slice(half * SUB // 2, (half + 1) * SUB // 2)
+            nc.sync.dma_start(out=x_sb[0][:, rows, :], in_=x_chunks[0][:, rows, :])
         load_c(0)
         load_c(1)
         nc.sync.dma_start(out=x_sb[1][:], in_=x_chunks[1])
@@ -190,39 +192,41 @@ def tile_chebykanprojector_pa_t_kernel(
                 in_=live[(name, c)][:].rearrange("p a g -> p (a g)") if count > 1 else live[(name, c)][:],
             )
 
-        def multiply(c, ot):
+        def multiply_base(c, ot):
             if not is_chunk(c):
                 return
-            codes = live[("codes", c)]
-            planes = live[("planes", c)]
             base_ps = psum.tile([P, ROWS], F32, name="base_ps")
-            poly_ps = psum.tile([P, ROWS], F32, name="poly_ps")
             live[("base_ps", c, ot)] = base_ps
-            live[("poly_ps", c, ot)] = poly_ps
             nc.tensor.matmul_mx(
                 out=base_ps[:],
                 lhsT=w_words[:, 2 * P * ot : 2 * P * (ot + 1)].bitcast(FP4X4),
                 lhsT_scale=w_plane[:, ot * P : (ot + 1) * P],
-                rhs=codes[:, 0, :].bitcast(FP8X4),
-                rhs_scale=planes[:, 0, :],
+                rhs=live[("codes", c)][:, 0, :].bitcast(FP8X4),
+                rhs_scale=live[("planes", c)][:, 0, :],
                 start=True,
                 stop=True,
             )
-            for d in range(DEG):
+
+        def multiply_poly(c, ot, first, last):
+            if not is_chunk(c):
+                return
+            if first == 1:
+                live[("poly_ps", c, ot)] = psum.tile([P, ROWS], F32, name="poly_ps")
+            for d in range(first, last + 1):
                 nc.tensor.matmul_mx(
-                    out=poly_ps[:],
-                    lhsT=c_codes[:, ot, d, :].bitcast(FP8X4),
-                    lhsT_scale=c_planes[:, ot, d, :],
-                    rhs=codes[:, d + 1, :].bitcast(FP8X4),
-                    rhs_scale=planes[:, d + 1, :],
-                    start=(d == 0),
-                    stop=(d == DEG - 1),
+                    out=live[("poly_ps", c, ot)][:],
+                    lhsT=c_codes[:, ot, d - 1, :].bitcast(FP8X4),
+                    lhsT_scale=c_planes[:, ot, d - 1, :],
+                    rhs=live[("codes", c)][:, d, :].bitcast(FP8X4),
+                    rhs_scale=live[("planes", c)][:, d, :],
+                    start=(d == 1),
+                    stop=(d == DEG),
                 )
 
         def add_bias(c, ot):
             if not is_chunk(c):
                 return
-            base_sb = double.tile([P, ROWS], F32, name="base_sb")
+            base_sb = double.tile([P, ROWS], F32, name="base_sb", bufs=3)
             live[("base_sb", c, ot)] = base_sb
             nc.scalar.activation(
                 out=base_sb[:], in_=live[("base_ps", c, ot)][:], func=ACT.Identity,
@@ -302,17 +306,19 @@ def tile_chebykanprojector_pa_t_kernel(
             nc.vector.tensor_tensor(out=bias_cols[:], in0=bias_cols[:], in1=b1_cols, op=ALU.add)
 
         for p in range(-2, N_CHUNKS + 3):
-            transpose_out(p - 3, 2)
-            transpose_out(p - 3, 3)
-            transpose_x(p + 1)
             if p == 1:
                 regroup_c(2, "scalar")
             tanh(p)
             cheby_3(p - 1)
-            multiply(p - 2, 2)
-            copy_out(p - 3, 2)
+            transpose_out(p - 3, 0)
+            transpose_out(p - 3, 1)
+            multiply_poly(p - 2, 2, 1, DEG)
             add_bias(p - 2, 2)
+            copy_out(p - 3, 0)
+            copy_out(p - 3, 1)
             combine(p - 2, 1)
+            multiply_base(p - 1, 0)
+            multiply_poly(p - 2, 3, 1, DEG)
             cheby_1(p)
             if p == 0:
                 regroup_c(1, "vector")
@@ -321,37 +327,38 @@ def tile_chebykanprojector_pa_t_kernel(
                 make_bias()
             quantise(p - 1, "t2", 2, 1)
             cheby_4(p - 1)
-
-            multiply(p - 2, 3)
             square_1(p)
-            add_bias(p - 2, 3)
-            copy_out(p - 3, 3)
-            combine(p - 2, 2)
-            quantise(p, "x_t1", 0, 2)
-            copy_x(p + 1, 0, "vector")
-            copy_x(p + 1, 1, "scalar")
-            quantise(p - 1, "t3_t4", 3, 2)
-            if p == -1:
-                regroup_c(0, "vector")
-                quantise_c(0)
+
+            transpose_out(p - 3, 2)
+            transpose_out(p - 3, 3)
+            transpose_x(p + 1)
             if p == 0:
                 sum_vectors()
+            combine(p - 2, 2)
+            multiply_poly(p - 1, 0, 1, 2)
+            quantise(p, "x_t1", 0, 2)
+            add_bias(p - 2, 3)
+            copy_out(p - 3, 2)
+            copy_out(p - 3, 3)
+            multiply_base(p - 1, 1)
+            add_bias(p - 1, 0)
+            quantise(p - 1, "t3_t4", 3, 2)
             if p == 1:
                 quantise_c(2)
                 regroup_c(3, "scalar")
-
-            multiply(p - 1, 0)
-            square_2(p)
-            add_bias(p - 1, 0)
+            multiply_poly(p - 1, 0, 3, DEG)
+            multiply_base(p - 1, 2)
+            copy_x(p + 1, 0, "vector")
+            copy_x(p + 1, 1, "scalar")
+            if p == -1:
+                regroup_c(0, "vector")
+                quantise_c(0)
             combine(p - 2, 3)
-            transpose_out(p - 2, 0)
-            copy_out(p - 2, 0)
-            transpose_out(p - 2, 1)
-            copy_out(p - 2, 1)
+            multiply_poly(p - 1, 1, 1, DEG)
+            square_2(p)
             cheby_2(p)
-
-            multiply(p - 1, 1)
-            add_bias(p - 1, 1)
             if p == 1:
                 quantise_c(3)
             combine(p - 1, 0)
+            add_bias(p - 1, 1)
+            multiply_base(p - 1, 3)

@@ -22,6 +22,9 @@ N_CHUNKS = B // ROWS
 O_TILES = H // P
 GROUPED = ROWS * PACK
 N_OPERANDS = DEG + 1
+TP_BANKS = 3
+POLY_BANKS = 3
+T2_ON_GPSIMD = True
 ONES_COLS = 32
 
 FLOPS = 2 * B * H * (IN + DEG * IN)
@@ -60,6 +63,7 @@ def tile_chebykanprojector_pa_t_kernel(
         vec_cols = keep.tile([P, 2 * O_TILES], F32)
         bias_cols = keep.tile([P, O_TILES], F32)
         ident = keep.tile([P, P], F32)
+        ident_bf = keep.tile([P, P], BF16)
         ones = keep.tile([P, ONES_COLS], BF16)
         warm = keep.tile([P, 1], F32)
         b1_cols = vec_cols[:, 0:O_TILES]
@@ -71,6 +75,7 @@ def tile_chebykanprojector_pa_t_kernel(
         nc.vector.memset(vec_rows[:], 0.0)
         nc.vector.memset(ones[:], 1.0)
         make_identity(nc, ident[:])
+        make_identity(nc, ident_bf[:])
 
         def load_c(ot):
             o_cols = slice(ot * P, (ot + 1) * P)
@@ -106,7 +111,7 @@ def tile_chebykanprojector_pa_t_kernel(
             if not is_chunk(c):
                 return
             for half in range(SUB // 2):
-                xt = psum.tile([P, 2, 2, P], F32, name="xt", tag="tp", bufs=4)
+                xt = psum.tile([P, 2, 2, P], F32, name="xt", tag="tp", bufs=TP_BANKS)
                 live[("xt", c, half)] = xt
                 for jj in range(2):
                     x_words = x_sb[c][:, 2 * half + jj, :].bitcast(F32)
@@ -153,11 +158,12 @@ def tile_chebykanprojector_pa_t_kernel(
                 return
             nc.vector.tensor_copy(out=live[("x_t1", c)][:, 1, :], in_=live[("t32", c)][:])
 
-        def cheby_2(c):
+        def cheby_2(c, on_gpsimd=True):
             if not is_chunk(c):
                 return
             live[("t2", c)] = single.tile([P, GROUPED], BF16, name="t2", align_bytes=64)
-            nc.vector.tensor_scalar(
+            engine = nc.gpsimd if (T2_ON_GPSIMD and on_gpsimd) else nc.vector
+            engine.tensor_scalar(
                 out=live[("t2", c)][:], in0=live[("w32", c)][:],
                 scalar1=0.5, scalar2=-1.0, op0=ALU.mult, op1=ALU.add,
             )
@@ -171,25 +177,36 @@ def tile_chebykanprojector_pa_t_kernel(
                 in1=live[("t32", c)][:], op0=ALU.subtract, op1=ALU.mult,
             )
 
-        def cheby_4(c):
+        def cheby_4(c, engine="vector"):
             if not is_chunk(c):
                 return
-            nc.vector.tensor_scalar(
-                out=live[("t3_t4", c)][:, 1, :], in0=live[("q32", c)][:],
-                scalar1=2.0, scalar2=-1.0, op0=ALU.mult, op1=ALU.add,
-            )
+            if engine == "vector":
+                nc.vector.tensor_scalar(
+                    out=live[("t3_t4", c)][:, 1, :], in0=live[("q32", c)][:],
+                    scalar1=2.0, scalar2=-1.0, op0=ALU.mult, op1=ALU.add,
+                )
+            else:
+                nc.scalar.activation(
+                    out=live[("t3_t4", c)][:, 1, :], in_=live[("q32", c)][:], func=ACT.Identity, scale=2.0, bias=-1.0
+                )
 
-        def quantise(c, name, first, count):
+        def quantise(c, name, first, count, slot=None):
             if not is_chunk(c):
                 return
             if first == 0:
                 live[("codes", c)] = double.tile([P, N_OPERANDS, ROWS], U32, name="codes", align_bytes=64)
                 live[("planes", c)] = double.tile([P, N_OPERANDS, ROWS], U8, name="planes", align_bytes=64)
             which = slice(first, first + count)
+            if slot is not None:
+                values = live[(name, c)][:, slot, :]
+            elif count > 1:
+                values = live[(name, c)][:].rearrange("p a g -> p (a g)")
+            else:
+                values = live[(name, c)][:]
             nc.vector.quantize_mx(
                 out=live[("codes", c)][:, which, :].rearrange("p a r -> p (a r)").bitcast(FP8X4),
                 scales=live[("planes", c)][:, which, :].rearrange("p a r -> p (a r)"),
-                in_=live[(name, c)][:].rearrange("p a g -> p (a g)") if count > 1 else live[(name, c)][:],
+                in_=values,
             )
 
         def multiply_base(c, ot):
@@ -207,12 +224,15 @@ def tile_chebykanprojector_pa_t_kernel(
                 stop=True,
             )
 
-        def multiply_poly(c, ot, first, last):
+        def multiply_poly(c, ot, degrees, stop_at=2, spare_bank=False):
             if not is_chunk(c):
                 return
-            if first == 1:
-                live[("poly_ps", c, ot)] = psum.tile([P, ROWS], F32, name="poly_ps")
-            for d in range(first, last + 1):
+            if degrees[0] == 1:
+                if spare_bank:
+                    live[("poly_ps", c, ot)] = psum.tile([P, ROWS], F32, name="poly_spare", tag="base_ps")
+                else:
+                    live[("poly_ps", c, ot)] = psum.tile([P, ROWS], F32, name="poly_ps", bufs=POLY_BANKS)
+            for d in degrees:
                 nc.tensor.matmul_mx(
                     out=live[("poly_ps", c, ot)][:],
                     lhsT=c_codes[:, ot, d - 1, :].bitcast(FP8X4),
@@ -220,13 +240,13 @@ def tile_chebykanprojector_pa_t_kernel(
                     rhs=live[("codes", c)][:, d, :].bitcast(FP8X4),
                     rhs_scale=live[("planes", c)][:, d, :],
                     start=(d == 1),
-                    stop=(d == DEG),
+                    stop=(d == stop_at),
                 )
 
         def add_bias(c, ot):
             if not is_chunk(c):
                 return
-            base_sb = double.tile([P, ROWS], F32, name="base_sb", bufs=3)
+            base_sb = double.tile([P, ROWS], F32, name="base_sb", bufs=6)
             live[("base_sb", c, ot)] = base_sb
             nc.scalar.activation(
                 out=base_sb[:], in_=live[("base_ps", c, ot)][:], func=ACT.Identity,
@@ -250,7 +270,7 @@ def tile_chebykanprojector_pa_t_kernel(
         def transpose_out(c, j):
             if not is_chunk(c):
                 return
-            out_ps = psum.tile([P, H], F32, name="out_ps", tag="tp", bufs=4)
+            out_ps = psum.tile([P, H], F32, name="out_ps", tag="tp", bufs=TP_BANKS)
             live[("out_ps", c, j)] = out_ps
             for ot in range(O_TILES):
                 nc.tensor.transpose(
@@ -259,20 +279,50 @@ def tile_chebykanprojector_pa_t_kernel(
                     ident[:],
                 )
 
-        def copy_out(c, j):
+        def transpose_out_tile(c, ot):
+            for j in range(SUB):
+                if ot == 0:
+                    if j < TP_BANKS:
+                        live[("out_ps", c, j)] = psum.tile([P, H], F32, name="out_ps", tag="tp", bufs=TP_BANKS)
+                    else:
+                        live[("out_ps", c, j)] = psum.tile([P, H], F32, name="out_spare", tag="base_ps")
+                nc.tensor.transpose(
+                    live[("out_ps", c, j)][:, ot * P : (ot + 1) * P],
+                    live[("sum_t", c)][:, ot, j * P : (j + 1) * P],
+                    ident[:],
+                )
+
+        def copy_out(c, j, engine="scalar"):
             if not is_chunk(c):
                 return
             if j == 0:
                 live[("out_sb", c)] = double.tile([P, SUB, H], F32, name="out_sb")
-            nc.scalar.copy(out=live[("out_sb", c)][:, j, :], in_=live[("out_ps", c, j)][:])
+            if engine == "vector":
+                nc.vector.tensor_copy(out=live[("out_sb", c)][:, j, :], in_=live[("out_ps", c, j)][:])
+            else:
+                nc.scalar.copy(out=live[("out_sb", c)][:, j, :], in_=live[("out_ps", c, j)][:])
             nc.sync.dma_start(out=out_chunks[c][:, j, :], in_=live[("out_sb", c)][:, j, :])
 
-        def regroup_c(ot, engine):
-            c_view = c_raw[:, :, ot * P : (ot + 1) * P, 1 : DEG + 1].rearrange("p t o d -> p d o t")
+        def regroup_c(ot):
+            for pair in range(DEG // 2):
+                cg_ps = psum.tile([P, 2, P, PACK], BF16, name="cg_ps", tag="poly_ps", bufs=POLY_BANKS)
+                live[("cg_ps", ot, pair)] = cg_ps
+                for e in range(2):
+                    nc.tensor.matmul(
+                        out=cg_ps[:, e],
+                        lhsT=ident_bf[:],
+                        rhs=c_raw[:, :, ot * P : (ot + 1) * P, 1 + 2 * pair + e].rearrange("p t o -> p o t"),
+                        start=True,
+                        stop=True,
+                    )
+
+        def copy_c(ot, pair, engine):
+            c_out = c_grouped[ot][:, 2 * pair : 2 * pair + 2].rearrange("p d o t -> p (d o t)")
+            c_in = live[("cg_ps", ot, pair)][:].rearrange("p e o t -> p (e o t)")
             if engine == "vector":
-                nc.vector.tensor_copy(out=c_grouped[ot][:], in_=c_view)
+                nc.vector.tensor_copy(out=c_out, in_=c_in)
             else:
-                nc.scalar.copy(out=c_grouped[ot][:], in_=c_view)
+                nc.scalar.copy(out=c_out, in_=c_in)
 
         def quantise_c(ot):
             nc.vector.quantize_mx(
@@ -281,12 +331,14 @@ def tile_chebykanprojector_pa_t_kernel(
                 in_=c_grouped[ot][:].rearrange("p d o t -> p (d o t)"),
             )
 
-        def sum_vectors():
+        def widen_vectors():
             nc.vector.tensor_copy(out=vec_f32[:], in_=vec_rows[:])
-            vec_ps = psum.tile([P, P], F32, name="vec_ps", tag="tp", bufs=4)
+
+        def sum_vectors():
+            vec_ps = psum.tile([P, P], F32, name="vec_ps", tag="tp", bufs=TP_BANKS)
             live[("vec_ps", 0)] = vec_ps
             nc.tensor.transpose(vec_ps[:], vec_f32[:], ident[:])
-            c0_ps = psum.tile([P, O_TILES, ONES_COLS], F32, name="c0_ps", tag="tp", bufs=4)
+            c0_ps = psum.tile([P, O_TILES, ONES_COLS], F32, name="c0_ps", tag="tp", bufs=TP_BANKS)
             live[("c0_ps", 0)] = c0_ps
             for ot in range(O_TILES):
                 for t in range(PACK):
@@ -305,60 +357,142 @@ def tile_chebykanprojector_pa_t_kernel(
             )
             nc.vector.tensor_tensor(out=bias_cols[:], in0=bias_cols[:], in1=b1_cols, op=ALU.add)
 
-        for p in range(-2, N_CHUNKS + 3):
-            if p == 1:
-                regroup_c(2, "scalar")
+        LAST = N_CHUNKS - 1
+        for p in range(-1, LAST):
             tanh(p)
-            cheby_3(p - 1)
-            transpose_out(p - 3, 0)
-            transpose_out(p - 3, 1)
-            multiply_poly(p - 2, 2, 1, DEG)
-            add_bias(p - 2, 2)
-            copy_out(p - 3, 0)
-            copy_out(p - 3, 1)
-            combine(p - 2, 1)
-            multiply_base(p - 1, 0)
-            multiply_poly(p - 2, 3, 1, DEG)
+            cheby_4(p - 1)
+            if p == 1:
+                add_bias(0, 2)
+                add_bias(0, 3)
+                multiply_base(1, 0)
+                multiply_base(1, 1)
+            transpose_x(p + 1)
+            quantise(p - 1, "t3_t4", 3, 2)
+            square_1(p)
             cheby_1(p)
             if p == 0:
-                regroup_c(1, "vector")
-                quantise_c(1)
-            if p == 1:
-                make_bias()
-            quantise(p - 1, "t2", 2, 1)
-            cheby_4(p - 1)
-            square_1(p)
-
-            transpose_out(p - 3, 2)
-            transpose_out(p - 3, 3)
-            transpose_x(p + 1)
-            if p == 0:
-                sum_vectors()
-            combine(p - 2, 2)
-            multiply_poly(p - 1, 0, 1, 2)
-            quantise(p, "x_t1", 0, 2)
-            add_bias(p - 2, 3)
-            copy_out(p - 3, 2)
-            copy_out(p - 3, 3)
-            multiply_base(p - 1, 1)
-            add_bias(p - 1, 0)
-            quantise(p - 1, "t3_t4", 3, 2)
-            if p == 1:
-                quantise_c(2)
-                regroup_c(3, "scalar")
-            multiply_poly(p - 1, 0, 3, DEG)
-            multiply_base(p - 1, 2)
-            copy_x(p + 1, 0, "vector")
-            copy_x(p + 1, 1, "scalar")
-            if p == -1:
-                regroup_c(0, "vector")
+                widen_vectors()
                 quantise_c(0)
-            combine(p - 2, 3)
-            multiply_poly(p - 1, 1, 1, DEG)
-            square_2(p)
+                regroup_c(2)
+            for ot in range(3):
+                multiply_poly(p - 1, ot, [3, 4])
+            quantise(p - 1, "t2", 2, 1)
+            if p > 0:
+                add_bias(p, 0)
+                add_bias(p, 1)
             cheby_2(p)
-            if p == 1:
-                quantise_c(3)
+            if p == 0:
+                copy_c(1, 0, "vector")
+                copy_c(1, 1, "vector")
+            copy_x(p + 1, 0, "vector")
+            for ot in range(3):
+                multiply_poly(p - 1, ot, [2])
             combine(p - 1, 0)
-            add_bias(p - 1, 1)
-            multiply_base(p - 1, 3)
+            copy_x(p + 1, 1, "scalar" if p == -1 else "vector")
+            multiply_poly(p - 1, 3, [1, 3, 4, 2])
+            square_2(p)
+            combine(p - 1, 1)
+            combine(p - 1, 2)
+            if p > 0:
+                multiply_base(p, 2)
+                multiply_base(p, 3)
+            combine(p - 1, 3)
+            if p == -1:
+                regroup_c(0)
+            if p == 0:
+                copy_c(2, 0, "scalar")
+                regroup_c(3)
+                copy_c(2, 1, "scalar")
+                sum_vectors()
+                multiply_base(0, 0)
+                multiply_base(0, 1)
+                quantise_c(1)
+                quantise(1, "x_t1", 0, 1, slot=0)
+                make_bias()
+                copy_c(3, 0, "scalar")
+                copy_c(3, 1, "scalar")
+                add_bias(0, 0)
+                add_bias(0, 1)
+                multiply_base(0, 2)
+                multiply_base(0, 3)
+            if p > 0:
+                add_bias(p, 2)
+                add_bias(p, 3)
+            if p != 0:
+                quantise(p + 1, "x_t1", 0, 1, slot=0)
+            transpose_out(p - 1, 0)
+            transpose_out(p - 1, 1)
+            transpose_out(p - 1, 2)
+            if p == -1:
+                copy_c(0, 0, "vector")
+                copy_c(0, 1, "vector")
+                regroup_c(1)
+            quantise(p, "x_t1", 1, 1, slot=1)
+            if p > 0:
+                multiply_base(p + 1, 0)
+                multiply_base(p + 1, 1)
+            copy_out(p - 1, 0)
+            transpose_out(p - 1, 3)
+            cheby_3(p)
+            if p == 0:
+                quantise_c(2)
+                quantise_c(3)
+            for ot in range(3):
+                multiply_poly(p, ot, [1])
+            copy_out(p - 1, 1)
+            copy_out(p - 1, 2)
+            copy_out(p - 1, 3)
+
+        p = LAST
+        tanh(p)
+        cheby_4(p - 1)
+        quantise(p - 1, "t3_t4", 3, 2)
+        square_1(p)
+        cheby_1(p)
+        for ot in range(3):
+            multiply_poly(p - 1, ot, [3, 4])
+        quantise(p - 1, "t2", 2, 1)
+        quantise(p, "x_t1", 1, 1, slot=1)
+        add_bias(p, 0)
+        add_bias(p, 1)
+        cheby_2(p)
+        for ot in range(3):
+            multiply_poly(p - 1, ot, [2])
+        combine(p - 1, 0)
+        multiply_poly(p - 1, 3, [1, 3, 4, 2])
+        square_2(p)
+        combine(p - 1, 1)
+        combine(p - 1, 2)
+        multiply_base(p, 2)
+        multiply_base(p, 3)
+        multiply_poly(p, 0, [1], stop_at=3)
+        multiply_poly(p, 1, [1], stop_at=3)
+        combine(p - 1, 3)
+        quantise(p, "t2", 2, 1)
+        transpose_out(p - 1, 0)
+        transpose_out(p - 1, 1)
+        transpose_out(p - 1, 2)
+        multiply_poly(p, 2, [1], stop_at=3)
+        cheby_3(p)
+        cheby_4(p, "scalar")
+        for ot in range(3):
+            multiply_poly(p, ot, [2], stop_at=3)
+        copy_out(p - 1, 0)
+        transpose_out(p - 1, 3)
+        add_bias(p, 2)
+        add_bias(p, 3)
+        quantise(p, "t3_t4", 4, 1, slot=1)
+        for ot in range(3):
+            multiply_poly(p, ot, [4], stop_at=3)
+        copy_out(p - 1, 1)
+        quantise(p, "t3_t4", 3, 1, slot=0)
+        copy_out(p - 1, 2)
+        copy_out(p - 1, 3)
+        for ot in range(3):
+            multiply_poly(p, ot, [3], stop_at=3)
+        multiply_poly(p, 3, [1, 2, 4, 3], stop_at=3, spare_bank=True)
+        for ot in range(O_TILES):
+            combine(p, ot)
+            transpose_out_tile(p, ot)
+        for j in range(SUB):
+            copy_out(p, j, "scalar" if j % 2 == 0 else "vector")

@@ -22,8 +22,8 @@ N_CHUNKS = B // ROWS
 O_TILES = H // P
 GROUPED = ROWS * PACK
 N_OPERANDS = DEG + 1
-TP_BANKS = 3
-POLY_BANKS = 3
+TP_BANKS = 4
+POLY_BANKS = 4
 T2_ON_GPSIMD = True
 ONES_COLS = 32
 
@@ -212,7 +212,7 @@ def tile_chebykanprojector_pa_t_kernel(
         def multiply_base(c, ot):
             if not is_chunk(c):
                 return
-            base_ps = psum.tile([P, ROWS], F32, name="base_ps")
+            base_ps = psum.tile([P, ROWS], F32, name="base_ps", tag="tp", bufs=TP_BANKS)
             live[("base_ps", c, ot)] = base_ps
             nc.tensor.matmul_mx(
                 out=base_ps[:],
@@ -224,14 +224,11 @@ def tile_chebykanprojector_pa_t_kernel(
                 stop=True,
             )
 
-        def multiply_poly(c, ot, degrees, stop_at=2, spare_bank=False):
+        def multiply_poly(c, ot, degrees, stop_at=2):
             if not is_chunk(c):
                 return
             if degrees[0] == 1:
-                if spare_bank:
-                    live[("poly_ps", c, ot)] = psum.tile([P, ROWS], F32, name="poly_spare", tag="base_ps")
-                else:
-                    live[("poly_ps", c, ot)] = psum.tile([P, ROWS], F32, name="poly_ps", bufs=POLY_BANKS)
+                live[("poly_ps", c, ot)] = psum.tile([P, ROWS], F32, name="poly_ps", bufs=POLY_BANKS)
             for d in degrees:
                 nc.tensor.matmul_mx(
                     out=live[("poly_ps", c, ot)][:],
@@ -282,10 +279,7 @@ def tile_chebykanprojector_pa_t_kernel(
         def transpose_out_tile(c, ot):
             for j in range(SUB):
                 if ot == 0:
-                    if j < TP_BANKS:
-                        live[("out_ps", c, j)] = psum.tile([P, H], F32, name="out_ps", tag="tp", bufs=TP_BANKS)
-                    else:
-                        live[("out_ps", c, j)] = psum.tile([P, H], F32, name="out_spare", tag="base_ps")
+                    live[("out_ps", c, j)] = psum.tile([P, H], F32, name="out_ps", tag="tp", bufs=TP_BANKS)
                 nc.tensor.transpose(
                     live[("out_ps", c, j)][:, ot * P : (ot + 1) * P],
                     live[("sum_t", c)][:, ot, j * P : (j + 1) * P],
@@ -364,9 +358,12 @@ def tile_chebykanprojector_pa_t_kernel(
             if p == 1:
                 add_bias(0, 2)
                 add_bias(0, 3)
-                multiply_base(1, 0)
-                multiply_base(1, 1)
-            transpose_x(p + 1)
+            if p > 0:
+                multiply_base(p, 0)
+                multiply_base(p, 1)
+            quantise(p - 1, "x_t1", 1, 1, slot=1)
+            for ot in range(O_TILES):
+                multiply_poly(p - 1, ot, [1])
             quantise(p - 1, "t3_t4", 3, 2)
             square_1(p)
             cheby_1(p)
@@ -374,29 +371,28 @@ def tile_chebykanprojector_pa_t_kernel(
                 widen_vectors()
                 quantise_c(0)
                 regroup_c(2)
-            for ot in range(3):
+            for ot in range(O_TILES):
                 multiply_poly(p - 1, ot, [3, 4])
             quantise(p - 1, "t2", 2, 1)
             if p > 0:
                 add_bias(p, 0)
                 add_bias(p, 1)
             cheby_2(p)
+            if p == -1:
+                transpose_x(0)
             if p == 0:
                 copy_c(1, 0, "vector")
                 copy_c(1, 1, "vector")
             copy_x(p + 1, 0, "vector")
-            for ot in range(3):
-                multiply_poly(p - 1, ot, [2])
-            combine(p - 1, 0)
             copy_x(p + 1, 1, "scalar" if p == -1 else "vector")
-            multiply_poly(p - 1, 3, [1, 3, 4, 2])
+            for ot in range(O_TILES):
+                multiply_poly(p - 1, ot, [2])
             square_2(p)
-            combine(p - 1, 1)
-            combine(p - 1, 2)
             if p > 0:
                 multiply_base(p, 2)
                 multiply_base(p, 3)
-            combine(p - 1, 3)
+            for ot in range(O_TILES):
+                combine(p - 1, ot)
             if p == -1:
                 regroup_c(0)
             if p == 0:
@@ -407,7 +403,8 @@ def tile_chebykanprojector_pa_t_kernel(
                 multiply_base(0, 0)
                 multiply_base(0, 1)
                 quantise_c(1)
-                quantise(1, "x_t1", 0, 1, slot=0)
+            quantise(p + 1, "x_t1", 0, 1, slot=0)
+            if p == 0:
                 make_bias()
                 copy_c(3, 0, "scalar")
                 copy_c(3, 1, "scalar")
@@ -418,79 +415,66 @@ def tile_chebykanprojector_pa_t_kernel(
             if p > 0:
                 add_bias(p, 2)
                 add_bias(p, 3)
-            if p != 0:
-                quantise(p + 1, "x_t1", 0, 1, slot=0)
-            transpose_out(p - 1, 0)
-            transpose_out(p - 1, 1)
-            transpose_out(p - 1, 2)
             if p == -1:
                 copy_c(0, 0, "vector")
                 copy_c(0, 1, "vector")
                 regroup_c(1)
-            quantise(p, "x_t1", 1, 1, slot=1)
-            if p > 0:
-                multiply_base(p + 1, 0)
-                multiply_base(p + 1, 1)
-            copy_out(p - 1, 0)
-            transpose_out(p - 1, 3)
+            for j in range(SUB):
+                transpose_out(p - 1, j)
+            transpose_x(p + 2)
             cheby_3(p)
             if p == 0:
                 quantise_c(2)
                 quantise_c(3)
-            for ot in range(3):
-                multiply_poly(p, ot, [1])
-            copy_out(p - 1, 1)
-            copy_out(p - 1, 2)
-            copy_out(p - 1, 3)
+            for j in range(SUB):
+                copy_out(p - 1, j)
 
         p = LAST
         tanh(p)
         cheby_4(p - 1)
+        multiply_base(p, 0)
+        multiply_base(p, 1)
+        quantise(p - 1, "x_t1", 1, 1, slot=1)
+        for ot in range(O_TILES):
+            multiply_poly(p - 1, ot, [1])
         quantise(p - 1, "t3_t4", 3, 2)
         square_1(p)
         cheby_1(p)
-        for ot in range(3):
+        for ot in range(O_TILES):
             multiply_poly(p - 1, ot, [3, 4])
         quantise(p - 1, "t2", 2, 1)
         quantise(p, "x_t1", 1, 1, slot=1)
         add_bias(p, 0)
         add_bias(p, 1)
         cheby_2(p)
-        for ot in range(3):
+        for ot in range(O_TILES):
             multiply_poly(p - 1, ot, [2])
-        combine(p - 1, 0)
-        multiply_poly(p - 1, 3, [1, 3, 4, 2])
         square_2(p)
-        combine(p - 1, 1)
-        combine(p - 1, 2)
         multiply_base(p, 2)
         multiply_base(p, 3)
-        multiply_poly(p, 0, [1], stop_at=3)
-        multiply_poly(p, 1, [1], stop_at=3)
-        combine(p - 1, 3)
+        for ot in range(O_TILES):
+            combine(p - 1, ot)
+        for ot in range(O_TILES):
+            multiply_poly(p, ot, [1], stop_at=3)
         quantise(p, "t2", 2, 1)
-        transpose_out(p - 1, 0)
-        transpose_out(p - 1, 1)
-        transpose_out(p - 1, 2)
-        multiply_poly(p, 2, [1], stop_at=3)
+        for j in range(SUB):
+            transpose_out(p - 1, j)
         cheby_3(p)
         cheby_4(p, "scalar")
-        for ot in range(3):
+        for ot in range(O_TILES):
             multiply_poly(p, ot, [2], stop_at=3)
-        copy_out(p - 1, 0)
-        transpose_out(p - 1, 3)
         add_bias(p, 2)
         add_bias(p, 3)
+        copy_out(p - 1, 0)
         quantise(p, "t3_t4", 4, 1, slot=1)
-        for ot in range(3):
+        for ot in range(O_TILES):
             multiply_poly(p, ot, [4], stop_at=3)
         copy_out(p - 1, 1)
         quantise(p, "t3_t4", 3, 1, slot=0)
         copy_out(p - 1, 2)
         copy_out(p - 1, 3)
-        for ot in range(3):
+        for ot in range(O_TILES):
             multiply_poly(p, ot, [3], stop_at=3)
-        multiply_poly(p, 3, [1, 2, 4, 3], stop_at=3, spare_bank=True)
         for ot in range(O_TILES):
             combine(p, ot)
             transpose_out_tile(p, ot)

@@ -63,7 +63,6 @@ def tile_chebykanprojector_pa_t_kernel(
         vec_cols = keep.tile([P, 2 * O_TILES], F32)
         bias_cols = keep.tile([P, O_TILES], F32)
         ident = keep.tile([P, P], F32)
-        ident_bf = keep.tile([P, P], BF16)
         ones = keep.tile([P, ONES_COLS], BF16)
         warm = keep.tile([P, 1], F32)
         b1_cols = vec_cols[:, 0:O_TILES]
@@ -75,7 +74,6 @@ def tile_chebykanprojector_pa_t_kernel(
         nc.vector.memset(vec_rows[:], 0.0)
         nc.vector.memset(ones[:], 1.0)
         make_identity(nc, ident[:])
-        make_identity(nc, ident_bf[:])
 
         def load_c(ot):
             o_cols = slice(ot * P, (ot + 1) * P)
@@ -297,26 +295,12 @@ def tile_chebykanprojector_pa_t_kernel(
                 nc.scalar.copy(out=live[("out_sb", c)][:, j, :], in_=live[("out_ps", c, j)][:])
             nc.sync.dma_start(out=out_chunks[c][:, j, :], in_=live[("out_sb", c)][:, j, :])
 
-        def regroup_c(ot):
-            for pair in range(DEG // 2):
-                cg_ps = psum.tile([P, 2, P, PACK], BF16, name="cg_ps", tag="poly_ps", bufs=POLY_BANKS)
-                live[("cg_ps", ot, pair)] = cg_ps
-                for e in range(2):
-                    nc.tensor.matmul(
-                        out=cg_ps[:, e],
-                        lhsT=ident_bf[:],
-                        rhs=c_raw[:, :, ot * P : (ot + 1) * P, 1 + 2 * pair + e].rearrange("p t o -> p o t"),
-                        start=True,
-                        stop=True,
-                    )
-
-        def copy_c(ot, pair, engine):
-            c_out = c_grouped[ot][:, 2 * pair : 2 * pair + 2].rearrange("p d o t -> p (d o t)")
-            c_in = live[("cg_ps", ot, pair)][:].rearrange("p e o t -> p (e o t)")
+        def regroup_c(ot, engine):
+            c_view = c_raw[:, :, ot * P : (ot + 1) * P, 1 : DEG + 1].rearrange("p t o d -> p d o t")
             if engine == "vector":
-                nc.vector.tensor_copy(out=c_out, in_=c_in)
+                nc.vector.tensor_copy(out=c_grouped[ot][:], in_=c_view)
             else:
-                nc.scalar.copy(out=c_out, in_=c_in)
+                nc.scalar.copy(out=c_grouped[ot][:], in_=c_view)
 
         def quantise_c(ot):
             nc.vector.quantize_mx(
@@ -370,7 +354,6 @@ def tile_chebykanprojector_pa_t_kernel(
             if p == 0:
                 widen_vectors()
                 quantise_c(0)
-                regroup_c(2)
             for ot in range(O_TILES):
                 multiply_poly(p - 1, ot, [3, 4])
             quantise(p - 1, "t2", 2, 1)
@@ -380,13 +363,12 @@ def tile_chebykanprojector_pa_t_kernel(
             cheby_2(p)
             if p == -1:
                 transpose_x(0)
-            if p == 0:
-                copy_c(1, 0, "vector")
-                copy_c(1, 1, "vector")
             copy_x(p + 1, 0, "vector")
             copy_x(p + 1, 1, "scalar" if p == -1 else "vector")
             for ot in range(O_TILES):
                 multiply_poly(p - 1, ot, [2])
+            if p == 0:
+                regroup_c(2, "scalar")
             square_2(p)
             if p > 0:
                 multiply_base(p, 2)
@@ -394,20 +376,17 @@ def tile_chebykanprojector_pa_t_kernel(
             for ot in range(O_TILES):
                 combine(p - 1, ot)
             if p == -1:
-                regroup_c(0)
+                regroup_c(0, "vector")
             if p == 0:
-                copy_c(2, 0, "scalar")
-                regroup_c(3)
-                copy_c(2, 1, "scalar")
+                regroup_c(1, "vector")
                 sum_vectors()
                 multiply_base(0, 0)
                 multiply_base(0, 1)
-                quantise_c(1)
             quantise(p + 1, "x_t1", 0, 1, slot=0)
             if p == 0:
                 make_bias()
-                copy_c(3, 0, "scalar")
-                copy_c(3, 1, "scalar")
+                quantise_c(1)
+                regroup_c(3, "scalar")
                 add_bias(0, 0)
                 add_bias(0, 1)
                 multiply_base(0, 2)
@@ -415,10 +394,6 @@ def tile_chebykanprojector_pa_t_kernel(
             if p > 0:
                 add_bias(p, 2)
                 add_bias(p, 3)
-            if p == -1:
-                copy_c(0, 0, "vector")
-                copy_c(0, 1, "vector")
-                regroup_c(1)
             for j in range(SUB):
                 transpose_out(p - 1, j)
             transpose_x(p + 2)

@@ -354,7 +354,7 @@ def tile_chebykanprojector_pa_t_kernel(
             if p == 0:
                 widen_vectors()
                 quantise_c(0)
-            for ot in range(O_TILES):
+            for ot in range(2):
                 multiply_poly(p - 1, ot, [3, 4])
             quantise(p - 1, "t2", 2, 1)
             if p > 0:
@@ -365,8 +365,10 @@ def tile_chebykanprojector_pa_t_kernel(
                 transpose_x(0)
             copy_x(p + 1, 0, "vector")
             copy_x(p + 1, 1, "scalar" if p == -1 else "vector")
-            for ot in range(O_TILES):
+            for ot in range(2):
                 multiply_poly(p - 1, ot, [2])
+            for ot in range(2, O_TILES):
+                multiply_poly(p - 1, ot, [3, 4, 2])
             if p == 0:
                 regroup_c(2, "scalar")
             square_2(p)
@@ -415,41 +417,45 @@ def tile_chebykanprojector_pa_t_kernel(
         quantise(p - 1, "t3_t4", 3, 2)
         square_1(p)
         cheby_1(p)
-        for ot in range(O_TILES):
+        for ot in range(2):
             multiply_poly(p - 1, ot, [3, 4])
         quantise(p - 1, "t2", 2, 1)
         quantise(p, "x_t1", 1, 1, slot=1)
         add_bias(p, 0)
         add_bias(p, 1)
         cheby_2(p)
-        for ot in range(O_TILES):
+        for ot in range(2):
             multiply_poly(p - 1, ot, [2])
+        for ot in range(2, O_TILES):
+            multiply_poly(p - 1, ot, [3, 4, 2])
         square_2(p)
         multiply_base(p, 2)
         multiply_base(p, 3)
         for ot in range(O_TILES):
             combine(p - 1, ot)
+        add_bias(p, 2)
+        add_bias(p, 3)
         for ot in range(O_TILES):
-            multiply_poly(p, ot, [1], stop_at=3)
+            multiply_poly(p, ot, [1], stop_at=4)
         quantise(p, "t2", 2, 1)
         for j in range(SUB):
             transpose_out(p - 1, j)
         cheby_3(p)
         cheby_4(p, "scalar")
         for ot in range(O_TILES):
-            multiply_poly(p, ot, [2], stop_at=3)
-        add_bias(p, 2)
-        add_bias(p, 3)
+            multiply_poly(p, ot, [2], stop_at=4)
         copy_out(p - 1, 0)
-        quantise(p, "t3_t4", 4, 1, slot=1)
-        for ot in range(O_TILES):
-            multiply_poly(p, ot, [4], stop_at=3)
-        copy_out(p - 1, 1)
         quantise(p, "t3_t4", 3, 1, slot=0)
+        for ot in range(2):
+            multiply_poly(p, ot, [3], stop_at=4)
+        copy_out(p - 1, 1)
+        quantise(p, "t3_t4", 4, 1, slot=1)
         copy_out(p - 1, 2)
         copy_out(p - 1, 3)
-        for ot in range(O_TILES):
-            multiply_poly(p, ot, [3], stop_at=3)
+        for ot in range(2):
+            multiply_poly(p, ot, [4], stop_at=4)
+        for ot in range(2, O_TILES):
+            multiply_poly(p, ot, [3, 4], stop_at=4)
         for ot in range(O_TILES):
             combine(p, ot)
             transpose_out_tile(p, ot)

@@ -274,15 +274,18 @@ def tile_chebykanprojector_pa_t_kernel(
                     ident[:],
                 )
 
-        def transpose_out_tile(c, ot):
+        def finish_tile(c, ot, engine):
+            out_ps = psum.tile([P, SUB, P], F32, name="out_ps", tag="tp", bufs=TP_BANKS)
             for j in range(SUB):
-                if ot == 0:
-                    live[("out_ps", c, j)] = psum.tile([P, H], F32, name="out_ps", tag="tp", bufs=TP_BANKS)
-                nc.tensor.transpose(
-                    live[("out_ps", c, j)][:, ot * P : (ot + 1) * P],
-                    live[("sum_t", c)][:, ot, j * P : (j + 1) * P],
-                    ident[:],
-                )
+                nc.tensor.transpose(out_ps[:, j, :], live[("sum_t", c)][:, ot, j * P : (j + 1) * P], ident[:])
+            if ot == 0:
+                live[("out_sb", c)] = double.tile([P, SUB, H], F32, name="out_sb")
+            o_cols = slice(ot * P, (ot + 1) * P)
+            if engine == "vector":
+                nc.vector.tensor_copy(out=live[("out_sb", c)][:, :, o_cols], in_=out_ps[:])
+            else:
+                nc.scalar.copy(out=live[("out_sb", c)][:, :, o_cols], in_=out_ps[:])
+            nc.sync.dma_start(out=out_chunks[c][:, :, o_cols], in_=live[("out_sb", c)][:, :, o_cols])
 
         def copy_out(c, j, engine="scalar"):
             if not is_chunk(c):
@@ -458,6 +461,4 @@ def tile_chebykanprojector_pa_t_kernel(
             multiply_poly(p, ot, [3, 4], stop_at=4)
         for ot in range(O_TILES):
             combine(p, ot)
-            transpose_out_tile(p, ot)
-        for j in range(SUB):
-            copy_out(p, j, "scalar" if j % 2 == 0 else "vector")
+            finish_tile(p, ot, "scalar")

@@ -299,11 +299,12 @@ def tile_chebykanprojector_pa_t_kernel(
             nc.sync.dma_start(out=out_chunks[c][:, j, :], in_=live[("out_sb", c)][:, j, :])
 
         def regroup_c(ot, engine):
-            c_view = c_raw[:, :, ot * P : (ot + 1) * P, 1 : DEG + 1].rearrange("p t o d -> p d o t")
+            c_in = c_raw[:, :, ot * P : (ot + 1) * P, 1 : DEG + 1].rearrange("p t o d -> p o t d")
+            c_out = c_grouped[ot][:].rearrange("p d o t -> p o t d")
             if engine == "vector":
-                nc.vector.tensor_copy(out=c_grouped[ot][:], in_=c_view)
+                nc.vector.tensor_copy(out=c_out, in_=c_in)
             else:
-                nc.scalar.copy(out=c_grouped[ot][:], in_=c_view)
+                nc.scalar.copy(out=c_out, in_=c_in)
 
         def quantise_c(ot):
             nc.vector.quantize_mx(

@@ -133,7 +133,10 @@ def tile_chebykanprojector_pa_t_kernel(
             if not is_chunk(c):
                 return
             live[("t32", c)] = double.tile([P, GROUPED], F32, name="t32")
-            nc.scalar.activation(out=live[("t32", c)][:], in_=live[("x_t1", c)][:, 0, :], func=ACT.Tanh)
+            pieces = 2 if c == 0 else 1
+            for piece in range(pieces):
+                cols = slice(piece * GROUPED // pieces, (piece + 1) * GROUPED // pieces)
+                nc.scalar.activation(out=live[("t32", c)][:, cols], in_=live[("x_t1", c)][:, 0, cols], func=ACT.Tanh)
 
         def square_1(c):
             if not is_chunk(c):
@@ -368,7 +371,7 @@ def tile_chebykanprojector_pa_t_kernel(
             if p == -1:
                 transpose_x(0)
             copy_x(p + 1, 0, "vector")
-            copy_x(p + 1, 1, "scalar" if p == -1 else "vector")
+            copy_x(p + 1, 1, "vector")
             for ot in range(2):
                 multiply_poly(p - 1, ot, [2])
             for ot in range(2, O_TILES):

from contextlib import ExitStack

import concourse.mybir as mybir
from concourse.masks import make_identity

F32 = mybir.dt.float32
BF16 = mybir.dt.bfloat16
I32 = mybir.dt.int32
U32 = mybir.dt.uint32
U8 = mybir.dt.uint8
FP8X4 = mybir.dt.float8_e4m3fn_x4
FP4X4 = mybir.dt.float4_e2m1fn_x4
ACT = mybir.ActivationFunctionType
ALU = mybir.AluOpType

P = 128
PACK = 4
B, IN, H, DEG = 4096, 512, 512, 4
ROWS = 512
SUB = ROWS // P
N_CHUNKS = B // ROWS
O_TILES = H // P
GROUPED = ROWS * PACK
N_OPERANDS = DEG + 1
TP_BANKS = 4
POLY_BANKS = 4
T2_ON_GPSIMD = True
ONES_COLS = 32

FLOPS = 2 * B * H * (IN + DEG * IN)


def tile_chebykanprojector_pa_t_kernel(
    tc, x, w1_base_words, w1_base_scales, b1_base, c1, s1, out
):
    nc = tc.nc
    x_chunks = x.rearrange("(c p j) k -> c p j k", p=P, j=SUB)
    out_chunks = out.rearrange("(c p j) o -> c p j o", p=P, j=SUB)
    c_by_partition = c1.rearrange("(p t) o d -> p t o d", t=PACK)

    with ExitStack() as ctx:
        ctx.enter_context(tc.manual_schedule())
        keep = ctx.enter_context(tc.tile_pool(name="keep", bufs=1))
        single = ctx.enter_context(tc.tile_pool(name="single", bufs=1))
        double = ctx.enter_context(tc.tile_pool(name="double", bufs=2))
        psum = ctx.enter_context(tc.psum_pool(name="psum", bufs=2))

        x_sb = []
        for c in range(N_CHUNKS):
            x_sb.append(keep.tile([P, SUB, IN], BF16, name="x_sb%d" % c))
        c_raw = keep.tile([P, PACK, H, DEG + 1], BF16)
        c_grouped = []
        for ot in range(O_TILES):
            c_grouped.append(
                keep.tile([P, DEG, P, PACK], BF16, name="c_grouped%d" % ot, align_bytes=64)
            )
        c_codes = keep.tile([P, O_TILES, DEG, P], U32, align_bytes=64)
        c_planes = keep.tile([P, O_TILES, DEG, P], U8, align_bytes=64)
        w_words = keep.tile([P, 2 * H], U8, align_bytes=64)
        w_plane = keep.tile([P, H], U8, align_bytes=64)
        vec_rows = keep.tile([P, P], BF16)
        vec_f32 = keep.tile([P, P], F32)
        vec_cols = keep.tile([P, 2 * O_TILES], F32)
        bias_cols = keep.tile([P, O_TILES], F32)
        ident = keep.tile([P, P], F32)
        ones = keep.tile([P, ONES_COLS], BF16)
        warm = keep.tile([P, 1], F32)
        b1_cols = vec_cols[:, 0:O_TILES]
        s1_cols = vec_cols[:, O_TILES : 2 * O_TILES]

        nc.vector.memset(warm[:], 0.0)
        nc.scalar.activation(out=warm[:], in_=warm[:], func=ACT.Tanh)
        nc.vector.memset(w_plane[:].bitcast(I32), 0)
        nc.vector.memset(vec_rows[:], 0.0)
        nc.vector.memset(ones[:], 1.0)
        make_identity(nc, ident[:])

        def load_c(ot):
            o_cols = slice(ot * P, (ot + 1) * P)
            nc.sync.dma_start(out=c_raw[:, :, o_cols, :], in_=c_by_partition[:, :, o_cols, :])

        for half in range(2):
            rows = slice(half * SUB // 2, (half + 1) * SUB // 2)
            nc.sync.dma_start(out=x_sb[0][:, rows, :], in_=x_chunks[0][:, rows, :])
        load_c(0)
        load_c(1)
        nc.sync.dma_start(out=x_sb[1][:], in_=x_chunks[1])
        nc.sync.dma_start(out=vec_rows[0:O_TILES, :], in_=b1_base.rearrange("(r o) -> r o", o=P))
        nc.sync.dma_start(
            out=vec_rows[O_TILES : 2 * O_TILES, :], in_=s1.rearrange("(r o) -> r o", o=P)
        )
        load_c(2)
        load_c(3)
        nc.sync.dma_start(out=w_words[:].bitcast(I32), in_=w1_base_words[0].bitcast(I32))
        for quad in range(4):
            nc.sync.dma_start(
                out=w_plane[32 * quad : 32 * quad + 4, :].bitcast(I32),
                in_=w1_base_scales[0, 4 * quad : 4 * quad + 4, :].bitcast(I32),
            )
        for c in range(2, N_CHUNKS):
            nc.sync.dma_start(out=x_sb[c][:], in_=x_chunks[c])

        live = {}

        def is_chunk(c):
            return 0 <= c < N_CHUNKS

        def transpose_x(c):
            if not is_chunk(c):
                return
            for half in range(SUB // 2):
                xt = psum.tile([P, 2, 2, P], F32, name="xt", tag="tp", bufs=TP_BANKS)
                live[("xt", c, half)] = xt
                for jj in range(2):
                    x_words = x_sb[c][:, 2 * half + jj, :].bitcast(F32)
                    for u in range(2):
                        nc.tensor.transpose(xt[:, jj, u, :], x_words[:, u : IN // 2 : 2], ident[:])

        def copy_x(c, half, engine):
            if not is_chunk(c):
                return
            if half == 0:
                live[("x_t1", c)] = double.tile([P, 2, GROUPED], BF16, name="x_t1", align_bytes=64)
            words_out = live[("x_t1", c)][:, 0, :].bitcast(F32)[:, half * 4 * P : (half + 1) * 4 * P]
            words_out = words_out.rearrange("p (j b u) -> p j b u", j=2, u=2)
            words_in = live[("xt", c, half)][:].rearrange("p j u b -> p j b u")
            if engine == "vector":
                nc.vector.tensor_copy(out=words_out, in_=words_in)
            else:
                nc.scalar.copy(out=words_out, in_=words_in)

        def tanh(c):
            if not is_chunk(c):
                return
            live[("t32", c)] = double.tile([P, GROUPED], F32, name="t32")
            pieces = 2 if c == 0 else 1
            for piece in range(pieces):
                cols = slice(piece * GROUPED // pieces, (piece + 1) * GROUPED // pieces)
                nc.scalar.activation(out=live[("t32", c)][:, cols], in_=live[("x_t1", c)][:, 0, cols], func=ACT.Tanh)

        def square_1(c):
            if not is_chunk(c):
                return
            live[("w32", c)] = double.tile([P, GROUPED], F32, name="w32")
            nc.scalar.activation(
                out=live[("w32", c)][:], in_=live[("t32", c)][:], func=ACT.Square, scale=2.0
            )

        def square_2(c):
            if not is_chunk(c):
                return
            live[("q32", c)] = double.tile([P, GROUPED], F32, name="q32")
            nc.scalar.activation(
                out=live[("q32", c)][:], in_=live[("w32", c)][:], func=ACT.Square, scale=0.5, bias=-1.0
            )

        def cheby_1(c):
            if not is_chunk(c):
                return
            nc.vector.tensor_copy(out=live[("x_t1", c)][:, 1, :], in_=live[("t32", c)][:])

        def cheby_2(c, on_gpsimd=True):
            if not is_chunk(c):
                return
            live[("t2", c)] = single.tile([P, GROUPED], BF16, name="t2", align_bytes=64)
            engine = nc.gpsimd if (T2_ON_GPSIMD and on_gpsimd) else nc.vector
            engine.tensor_scalar(
                out=live[("t2", c)][:], in0=live[("w32", c)][:],
                scalar1=0.5, scalar2=-1.0, op0=ALU.mult, op1=ALU.add,
            )

        def cheby_3(c):
            if not is_chunk(c):
                return
            live[("t3_t4", c)] = single.tile([P, 2, GROUPED], BF16, name="t3_t4", align_bytes=64)
            nc.vector.scalar_tensor_tensor(
                out=live[("t3_t4", c)][:, 0, :], in0=live[("w32", c)][:], scalar=3.0,
                in1=live[("t32", c)][:], op0=ALU.subtract, op1=ALU.mult,
            )

        def cheby_4(c, engine="vector"):
            if not is_chunk(c):
                return
            if engine == "vector":
                nc.vector.tensor_scalar(
                    out=live[("t3_t4", c)][:, 1, :], in0=live[("q32", c)][:],
                    scalar1=2.0, scalar2=-1.0, op0=ALU.mult, op1=ALU.add,
                )
            else:
                nc.scalar.activation(
                    out=live[("t3_t4", c)][:, 1, :], in_=live[("q32", c)][:], func=ACT.Identity, scale=2.0, bias=-1.0
                )

        def quantise(c, name, first, count, slot=None):
            if not is_chunk(c):
                return
            if first == 0:
                live[("codes", c)] = double.tile([P, N_OPERANDS, ROWS], U32, name="codes", align_bytes=64)
                live[("planes", c)] = double.tile([P, N_OPERANDS, ROWS], U8, name="planes", align_bytes=64)
            which = slice(first, first + count)
            if slot is not None:
                values = live[(name, c)][:, slot, :]
            elif count > 1:
                values = live[(name, c)][:].rearrange("p a g -> p (a g)")
            else:
                values = live[(name, c)][:]
            nc.vector.quantize_mx(
                out=live[("codes", c)][:, which, :].rearrange("p a r -> p (a r)").bitcast(FP8X4),
                scales=live[("planes", c)][:, which, :].rearrange("p a r -> p (a r)"),
                in_=values,
            )

        def multiply_base(c, ot):
            if not is_chunk(c):
                return
            base_ps = psum.tile([P, ROWS], F32, name="base_ps", tag="tp", bufs=TP_BANKS)
            live[("base_ps", c, ot)] = base_ps
            nc.tensor.matmul_mx(
                out=base_ps[:],
                lhsT=w_words[:, 2 * P * ot : 2 * P * (ot + 1)].bitcast(FP4X4),
                lhsT_scale=w_plane[:, ot * P : (ot + 1) * P],
                rhs=live[("codes", c)][:, 0, :].bitcast(FP8X4),
                rhs_scale=live[("planes", c)][:, 0, :],
                start=True,
                stop=True,
            )

        def multiply_poly(c, ot, degrees, stop_at=2):
            if not is_chunk(c):
                return
            if degrees[0] == 1:
                live[("poly_ps", c, ot)] = psum.tile([P, ROWS], F32, name="poly_ps", bufs=POLY_BANKS)
            for d in degrees:
                nc.tensor.matmul_mx(
                    out=live[("poly_ps", c, ot)][:],
                    lhsT=c_codes[:, ot, d - 1, :].bitcast(FP8X4),
                    lhsT_scale=c_planes[:, ot, d - 1, :],
                    rhs=live[("codes", c)][:, d, :].bitcast(FP8X4),
                    rhs_scale=live[("planes", c)][:, d, :],
                    start=(d == 1),
                    stop=(d == stop_at),
                )

        def add_bias(c, ot):
            if not is_chunk(c):
                return
            base_sb = double.tile([P, ROWS], F32, name="base_sb", bufs=6)
            live[("base_sb", c, ot)] = base_sb
            nc.scalar.activation(
                out=base_sb[:], in_=live[("base_ps", c, ot)][:], func=ACT.Identity,
                bias=bias_cols[:, ot : ot + 1], scale=1.0,
            )

        def combine(c, ot):
            if not is_chunk(c):
                return
            if ot == 0:
                live[("sum_t", c)] = double.tile([P, O_TILES, ROWS], F32, name="sum_t")
            nc.vector.scalar_tensor_tensor(
                out=live[("sum_t", c)][:, ot, :],
                in0=live[("poly_ps", c, ot)][:],
                scalar=s1_cols[:, ot : ot + 1],
                in1=live[("base_sb", c, ot)][:],
                op0=ALU.mult,
                op1=ALU.add,
            )

        def transpose_out(c, j):
            if not is_chunk(c):
                return
            out_ps = psum.tile([P, H], F32, name="out_ps", tag="tp", bufs=TP_BANKS)
            live[("out_ps", c, j)] = out_ps
            for ot in range(O_TILES):
                nc.tensor.transpose(
                    out_ps[:, ot * P : (ot + 1) * P],
                    live[("sum_t", c)][:, ot, j * P : (j + 1) * P],
                    ident[:],
                )

        def finish_tile(c, ot, engine):
            out_ps = psum.tile([P, SUB, P], F32, name="out_ps", tag="tp", bufs=TP_BANKS)
            for j in range(SUB):
                nc.tensor.transpose(out_ps[:, j, :], live[("sum_t", c)][:, ot, j * P : (j + 1) * P], ident[:])
            if ot == 0:
                live[("out_sb", c)] = double.tile([P, SUB, H], F32, name="out_sb")
            o_cols = slice(ot * P, (ot + 1) * P)
            if engine == "vector":
                nc.vector.tensor_copy(out=live[("out_sb", c)][:, :, o_cols], in_=out_ps[:])
            else:
                nc.scalar.copy(out=live[("out_sb", c)][:, :, o_cols], in_=out_ps[:])
            nc.sync.dma_start(out=out_chunks[c][:, :, o_cols], in_=live[("out_sb", c)][:, :, o_cols])

        def copy_out(c, j, engine="scalar"):
            if not is_chunk(c):
                return
            if j == 0:
                live[("out_sb", c)] = double.tile([P, SUB, H], F32, name="out_sb")
            if engine == "vector":
                nc.vector.tensor_copy(out=live[("out_sb", c)][:, j, :], in_=live[("out_ps", c, j)][:])
            else:
                nc.scalar.copy(out=live[("out_sb", c)][:, j, :], in_=live[("out_ps", c, j)][:])
            nc.sync.dma_start(out=out_chunks[c][:, j, :], in_=live[("out_sb", c)][:, j, :])

        def regroup_c(ot, engine):
            c_in = c_raw[:, :, ot * P : (ot + 1) * P, 1 : DEG + 1].rearrange("p t o d -> p o t d")
            c_out = c_grouped[ot][:].rearrange("p d o t -> p o t d")
            if engine == "vector":
                nc.vector.tensor_copy(out=c_out, in_=c_in)
            else:
                nc.scalar.copy(out=c_out, in_=c_in)

        def quantise_c(ot):
            nc.vector.quantize_mx(
                out=c_codes[:, ot].rearrange("p d o -> p (d o)").bitcast(FP8X4),
                scales=c_planes[:, ot].rearrange("p d o -> p (d o)"),
                in_=c_grouped[ot][:].rearrange("p d o t -> p (d o t)"),
            )

        def widen_vectors():
            nc.vector.tensor_copy(out=vec_f32[:], in_=vec_rows[:])

        def sum_vectors():
            vec_ps = psum.tile([P, P], F32, name="vec_ps", tag="tp", bufs=TP_BANKS)
            live[("vec_ps", 0)] = vec_ps
            nc.tensor.transpose(vec_ps[:], vec_f32[:], ident[:])
            c0_ps = psum.tile([P, O_TILES, ONES_COLS], F32, name="c0_ps", tag="tp", bufs=TP_BANKS)
            live[("c0_ps", 0)] = c0_ps
            for ot in range(O_TILES):
                for t in range(PACK):
                    nc.tensor.matmul(
                        out=c0_ps[:, ot, :],
                        lhsT=c_raw[:, t, ot * P : (ot + 1) * P, 0],
                        rhs=ones[:],
                        start=(t == 0),
                        stop=(t == PACK - 1),
                    )

        def make_bias():
            nc.vector.tensor_copy(out=vec_cols[:], in_=live[("vec_ps", 0)][:, 0 : 2 * O_TILES])
            nc.vector.tensor_tensor(
                out=bias_cols[:], in0=live[("c0_ps", 0)][:, :, 0], in1=s1_cols, op=ALU.mult
            )
            nc.vector.tensor_tensor(out=bias_cols[:], in0=bias_cols[:], in1=b1_cols, op=ALU.add)

        LAST = N_CHUNKS - 1
        for p in range(-1, LAST):
            tanh(p)
            cheby_4(p - 1)
            if p == 1:
                add_bias(0, 2)
                add_bias(0, 3)
            if p > 0:
                multiply_base(p, 0)
                multiply_base(p, 1)
            quantise(p - 1, "x_t1", 1, 1, slot=1)
            for ot in range(O_TILES):
                multiply_poly(p - 1, ot, [1])
            quantise(p - 1, "t3_t4", 3, 2)
            square_1(p)
            cheby_1(p)
            if p == 0:
                widen_vectors()
                quantise_c(0)
            for ot in range(2):
                multiply_poly(p - 1, ot, [3, 4])
            quantise(p - 1, "t2", 2, 1)
            if p > 0:
                add_bias(p, 0)
                add_bias(p, 1)
            cheby_2(p)
            if p == -1:
                transpose_x(0)
            copy_x(p + 1, 0, "vector")
            copy_x(p + 1, 1, "vector")
            for ot in range(2):
                multiply_poly(p - 1, ot, [2])
            for ot in range(2, O_TILES):
                multiply_poly(p - 1, ot, [3, 4, 2])
            if p == 0:
                regroup_c(2, "scalar")
            square_2(p)
            if p > 0:
                multiply_base(p, 2)
                multiply_base(p, 3)
            for ot in range(O_TILES):
                combine(p - 1, ot)
            if p == -1:
                regroup_c(0, "vector")
            if p == 0:
                regroup_c(1, "vector")
                sum_vectors()
                multiply_base(0, 0)
                multiply_base(0, 1)
            quantise(p + 1, "x_t1", 0, 1, slot=0)
            if p == 0:
                make_bias()
                quantise_c(1)
                regroup_c(3, "scalar")
                add_bias(0, 0)
                add_bias(0, 1)
                multiply_base(0, 2)
                multiply_base(0, 3)
            if p > 0:
                add_bias(p, 2)
                add_bias(p, 3)
            for j in range(SUB):
                transpose_out(p - 1, j)
            transpose_x(p + 2)
            cheby_3(p)
            if p == 0:
                quantise_c(2)
                quantise_c(3)
            for j in range(SUB):
                copy_out(p - 1, j)

        p = LAST
        tanh(p)
        cheby_4(p - 1)
        multiply_base(p, 0)
        multiply_base(p, 1)
        quantise(p - 1, "x_t1", 1, 1, slot=1)
        for ot in range(O_TILES):
            multiply_poly(p - 1, ot, [1])
        quantise(p - 1, "t3_t4", 3, 2)
        square_1(p)
        cheby_1(p)
        for ot in range(2):
            multiply_poly(p - 1, ot, [3, 4])
        quantise(p - 1, "t2", 2, 1)
        quantise(p, "x_t1", 1, 1, slot=1)
        add_bias(p, 0)
        add_bias(p, 1)
        cheby_2(p)
        for ot in range(2):
            multiply_poly(p - 1, ot, [2])
        for ot in range(2, O_TILES):
            multiply_poly(p - 1, ot, [3, 4, 2])
        square_2(p)
        multiply_base(p, 2)
        multiply_base(p, 3)
        for ot in range(O_TILES):
            combine(p - 1, ot)
        add_bias(p, 2)
        add_bias(p, 3)
        for ot in range(O_TILES):
            multiply_poly(p, ot, [1], stop_at=4)
        quantise(p, "t2", 2, 1)
        for j in range(SUB):
            transpose_out(p - 1, j)
        cheby_3(p)
        cheby_4(p, "scalar")
        for ot in range(O_TILES):
            multiply_poly(p, ot, [2], stop_at=4)
        copy_out(p - 1, 0)
        quantise(p, "t3_t4", 3, 1, slot=0)
        for ot in range(2):
            multiply_poly(p, ot, [3], stop_at=4)
        copy_out(p - 1, 1)
        quantise(p, "t3_t4", 4, 1, slot=1)
        copy_out(p - 1, 2)
        copy_out(p - 1, 3)
        for ot in range(2):
            multiply_poly(p, ot, [4], stop_at=4)
        for ot in range(2, O_TILES):
            multiply_poly(p, ot, [3, 4], stop_at=4)
        for ot in range(O_TILES):
            combine(p, ot)
            finish_tile(p, ot, "scalar")
